import numpy as np
import ml_dtypes


def mxq(x, axis, fmt="e4m3"):
    dtype, down = {"e4m3": (ml_dtypes.float8_e4m3fn, 7), "e5m2": (ml_dtypes.float8_e5m2, 14)}[fmt]
    v = np.moveaxis(np.asarray(x, np.float32).astype(ml_dtypes.bfloat16).astype(np.float64), axis, -1)
    blocks = v.reshape(v.shape[:-1] + (-1, 32))
    amax = np.abs(blocks).max(-1, keepdims=True)
    byte = np.maximum(np.where(amax > 0, np.frexp(amax)[1] - 1 + 127, 0) - down, 1)
    scale = np.exp2(byte - 127.0)
    codes = (blocks / scale).astype(np.float32).astype(dtype).astype(np.float64)
    return np.moveaxis((codes * scale).reshape(v.shape), -1, axis)


WIDE = False


def mx_kscale(k):
    if not WIDE:
        return np.ones(k)
    levels = np.array([10, -10, 5, -5, 0])
    if k % 512:
        return np.exp2(np.random.permutation(np.resize(levels, k // 32))).repeat(32)
    a = np.empty((k // 512, 16))
    for p in range(k // 512):
        a[p, :8] = np.random.permutation(np.resize(levels, 8))
        for g in range(8):
            far = levels[np.abs(levels - a[p, g]) >= 10]
            a[p, g + 8] = far[np.random.randint(len(far))]
    return np.exp2(a.ravel()).repeat(32)


BF16 = ml_dtypes.bfloat16


def bf(x):
    return np.asarray(x, np.float32).astype(BF16)


def f64(x):
    return np.asarray(x).astype(np.float64)


B, IN_F, OUT_F, N_ACT = 2048, 1024, 1024, 4


def sigmoid(v):
    return 1.0 / (1.0 + np.exp(-v))


def _cyclic_act_derivs(y):
    Bb, O = y.shape
    yg = y.reshape(Bb, O // N_ACT, N_ACT)
    th = np.tanh(yg[..., 0])
    sg = sigmoid(yg[..., 3])
    d = np.stack([
        1.0 - th * th,
        np.cos(yg[..., 1]),
        np.where(yg[..., 2] > 0.0, 1.0, 0.0),
        sg * (1.0 - sg),
    ], axis=-1)
    return d.reshape(Bb, O)


def setup_inputs():
    s = mx_kscale(B)[:, None]
    u = mx_kscale(OUT_F)
    limit = np.sqrt(6.0 / (IN_F + OUT_F))
    x0 = bf(np.random.standard_normal((B, IN_F)))
    W0 = bf(np.random.uniform(-limit, limit, (OUT_F, IN_F)))
    b = bf(np.random.standard_normal(OUT_F) * 0.1)
    g = bf(np.random.standard_normal((B, OUT_F)) * np.exp2(np.random.randint(-6, 1, (B, 1))) * 2.0 / s * u[None, :])
    y = f64(x0) @ f64(W0).T + f64(b)
    return {"input": bf(f64(x0) * s), "W": bf(f64(W0) / u[:, None]), "b": b,
            "y": np.asarray(y, np.float32), "grad_out": g}


def reference(input, W, b, y, grad_out):
    dy = f64(grad_out) * _cyclic_act_derivs(f64(y))
    dx = mxq(dy, 1, "e5m2") @ mxq(f64(W), 0, "e4m3")
    dW = mxq(dy, 0, "e5m2").T @ mxq(f64(input), 0, "e4m3")
    return dx, dW

@@ -1,0 +1,372 @@
+from contextlib import ExitStack
+import math
+
+import concourse.mybir as mybir
+from concourse.masks import make_identity
+
+B, IN_F, OUT_F = 2048, 1024, 1024
+FLOPS = 2 * 2 * B * IN_F * OUT_F
+BYTES = 2 * B * IN_F + 2 * OUT_F * IN_F + 4 * B * OUT_F + 2 * B * OUT_F + 4 * B * IN_F + 4 * OUT_F * IN_F
+
+F32 = mybir.dt.float32
+BF16 = mybir.dt.bfloat16
+I32 = mybir.dt.int32
+U32 = mybir.dt.uint32
+U8 = mybir.dt.uint8
+E4 = mybir.dt.float8_e4m3fn_x4
+E5 = mybir.dt.float8_e5m2_x4
+ACT = mybir.ActivationFunctionType
+ALU = mybir.AluOpType
+
+P = 128
+NG = 4
+NEG = (True, False, False, True)
+
+
+def tile_vdl_v_kernel(tc, x_in, w_in, b_in, y_in, g_in, out_0, out_1):
+    nc = tc.nc
+    y_v = y_in.rearrange("(G p j) w -> G p j w", p=P, j=4)
+    g_v = g_in.rearrange("(G p j) w -> G p j w", p=P, j=4)
+    x_v = x_in.rearrange("(G p j) w -> G p j w", p=P, j=4)
+    w_v = w_in.rearrange("(g q c t a) i -> g c a q t i", g=2, q=16, c=2, t=4, a=4)
+    o0_v = out_0.rearrange("(G p j) i -> G j p i", p=P, j=4)
+    o1_v = out_1.rearrange("(h m a) i -> h a m i", h=2, m=P, a=4)
+
+    with ExitStack() as ctx:
+        ctx.enter_context(tc.manual_schedule())
+        const = ctx.enter_context(tc.tile_pool(name="const", bufs=1))
+        keep = ctx.enter_context(tc.tile_pool(name="keep", bufs=1))
+        ypool = ctx.enter_context(tc.tile_pool(name="ypool", bufs=4))
+        gpool = ctx.enter_context(tc.tile_pool(name="gpool", bufs=4))
+        xpool = ctx.enter_context(tc.tile_pool(name="xpool", bufs=3))
+        epool = ctx.enter_context(tc.tile_pool(name="epool", bufs=2))
+        dpool = ctx.enter_context(tc.tile_pool(name="dpool", bufs=4))
+        ipool = ctx.enter_context(tc.tile_pool(name="ipool", bufs=3))
+        tpool = ctx.enter_context(tc.tile_pool(name="tpool", bufs=4))
+        cpool = ctx.enter_context(tc.tile_pool(name="cpool", bufs=3))
+        opool = ctx.enter_context(tc.tile_pool(name="opool", bufs=6))
+        ps = ctx.enter_context(tc.psum_pool(name="ps_a", bufs=4))
+        ps2 = ctx.enter_context(tc.psum_pool(name="ps_b", bufs=4))
+
+        warm = const.tile([P, 1], F32, name="warm")
+        warm2 = const.tile([P, 1], F32, name="warm2")
+        nc.vector.memset(warm[:], 0.0)
+        nc.scalar.activation(out=warm2[:], in_=warm[:], func=ACT.Silu)
+        ident = const.tile([P, P], F32, name="ident")
+        make_identity(nc, ident[:])
+        pidx = const.tile([P, 1], I32, name="pidx")
+        nc.gpsimd.iota(pidx[:], pattern=[[0, 1]], base=2, channel_multiplier=1)
+        pbit = const.tile([P, 1], I32, name="pbit")
+        nc.vector.tensor_scalar(out=pbit[:], in0=pidx[:], scalar1=1, scalar2=2,
+                                op0=ALU.logical_shift_right, op1=ALU.bitwise_and)
+        sgn = const.tile([P, 1], F32, name="sgn")
+        nc.vector.tensor_scalar(out=sgn[:], in0=pbit[:], scalar1=-1.0, scalar2=None, op0=ALU.add)
+
+        dyc = keep.tile([P, NG, OUT_F], U32, name="dyc", align_bytes=64)
+        dys = keep.tile([P, NG, OUT_F], U8, name="dys", align_bytes=64)
+        xc = keep.tile([P, NG, IN_F], U32, name="xc", align_bytes=64)
+        xs = keep.tile([P, NG, IN_F], U8, name="xs", align_bytes=64)
+        wc = keep.tile([P, 2, IN_F], U32, name="wc", align_bytes=64)
+        ws = keep.tile([P, 2, IN_F], U8, name="ws", align_bytes=64)
+
+        yts, gts, xts, wts, dyns, tcds, tscs, ets, tps, tis, ils = {}, {}, {}, {}, {}, {}, {}, {}, {}, {}, {}
+
+        def load_yg(s):
+            G, h = divmod(s, 2)
+            yt = ypool.tile([P, 2, OUT_F], F32, name="yt", tag="yt")
+            nc.sync.dma_start(out=yt[:], in_=y_v[G][:, 2 * h:2 * h + 2, :])
+            gt = gpool.tile([P, 2, OUT_F], BF16, name="gt", tag="gt")
+            nc.sync.dma_start(out=gt[:], in_=g_v[G][:, 2 * h:2 * h + 2, :])
+            yts[s] = yt[:].rearrange("p j w -> p (j w)")
+            gts[s] = gt[:].rearrange("p j w -> p (j w)")
+
+        def load_x(G):
+            xt = xpool.tile([P, 4, IN_F], BF16, name="xt", tag="xw")
+            nc.sync.dma_start(out=xt[:], in_=x_v[G])
+            xts[G] = xt
+
+        def load_w(g):
+            wt = xpool.tile([P, 4, IN_F], BF16, name="wt", tag="xw")
+            for a in range(4):
+                for c2 in range(2):
+                    nc.sync.dma_start(out=wt[2 * a + c2:P:8, :, :], in_=w_v[g, c2, a])
+            wts[g] = wt
+
+        def col(flat, a):
+            return flat[:, a:2048:4]
+
+        def runs(ap):
+            return ap.rearrange("p (n c) -> p n c", c=8)
+
+        def dst(s, a):
+            G, h = divmod(s, 2)
+            return dyns[G][:].rearrange("p j w -> p (j w)")[:, 2048 * h:2048 * (h + 1)].rearrange(
+                "p (n a c) -> p a n c", a=4, c=8)[:, a]
+
+        def e_alloc(s):
+            if s % 2 == 0:
+                dyn = dpool.tile([P, 4, OUT_F], BF16, name="dyn", tag="dyn", align_bytes=64)
+                dyns[s // 2] = dyn
+            t0 = epool.tile([P, 512], F32, name="t0", tag="t0")
+            t3 = epool.tile([P, 512], F32, name="t3", tag="t3")
+            kk = epool.tile([P, 512], I32, name="kk", tag="kk")
+            rr = epool.tile([P, 512], F32, name="rr", tag="rr")
+            ets[s] = (t0, t3, kk, rr)
+
+        def v_turns(s):
+            nc.vector.tensor_scalar(out=ets[s][2][:], in0=col(yts[s], 1), scalar1=1.0 / (2.0 * math.pi), scalar2=0.25,
+                                    op0=ALU.mult, op1=ALU.add)
+
+        def v_reduce(s):
+            nc.vector.scalar_tensor_tensor(out=ets[s][3][:], in0=ets[s][2][:], scalar=-2.0 * math.pi, in1=col(yts[s], 1),
+                                           op0=ALU.mult, op1=ALU.add)
+
+        def v_relu(s):
+            nc.vector.scalar_tensor_tensor(out=dst(s, 2), in0=runs(col(yts[s], 2)), scalar=0.0, in1=runs(col(gts[s], 2)),
+                                           op0=ALU.is_gt, op1=ALU.mult)
+
+        def s_tanh(s, a):
+            nc.scalar.activation(out=ets[s][0 if a == 0 else 1][:], in_=col(yts[s], a), func=ACT.Tanh,
+                                 scale=1.0 if a == 0 else 0.5)
+
+        def s_square(s, a):
+            t = ets[s][0 if a == 0 else 1]
+            nc.scalar.activation(out=t[:], in_=t[:], func=ACT.Square, scale=1.0 if a == 0 else 0.5)
+
+        def s_sin(s):
+            nc.scalar.activation(out=ets[s][3][:], in_=ets[s][3][:], func=ACT.Sin, bias=0.5 * math.pi)
+
+        def v_mul(s, a):
+            if a == 1:
+                nc.vector.tensor_tensor(out=dst(s, 1), in0=runs(ets[s][3][:]), in1=runs(col(gts[s], 1)), op=ALU.mult)
+            else:
+                nc.vector.scalar_tensor_tensor(out=dst(s, a), in0=runs(ets[s][0 if a == 0 else 1][:]),
+                                               scalar=1.0 if a == 0 else 0.25, in1=runs(col(gts[s], a)),
+                                               op0=ALU.subtract, op1=ALU.mult)
+
+        def il_w(g, ih, eng):
+            il = ipool.tile([P, 2048], BF16, name="il", tag="il", align_bytes=64)
+            ils[("w", g, ih)] = il
+            o = il[:].rearrange("p (i t) -> p i t", t=4)
+            i = wts[g][:, :, 512 * ih:512 * (ih + 1)].rearrange("p t i -> p i t")
+            if eng == "v":
+                nc.vector.tensor_scalar(out=o, in0=i, scalar1=sgn[:, 0:1], scalar2=None, op0=ALU.mult)
+            else:
+                nc.scalar.activation(out=o, in_=i, func=ACT.Copy, scale=sgn[:, 0:1])
+
+        def q_w(g, ih):
+            nc.vector.quantize_mx(out=wc[:, g, 512 * ih:512 * (ih + 1)].bitcast(E4),
+                                  scales=ws[:, g, 512 * ih:512 * (ih + 1)], in_=ils[("w", g, ih)][:])
+
+        def il_x(G, ih, eng):
+            il = ipool.tile([P, 2048], BF16, name="il", tag="il", align_bytes=64)
+            ils[("x", G, ih)] = il
+            o = il[:].rearrange("p (i j) -> p i j", j=4)
+            i = xts[G][:, :, 512 * ih:512 * (ih + 1)].rearrange("p j i -> p i j")
+            if eng == "v":
+                nc.vector.tensor_copy(out=o, in_=i)
+            else:
+                nc.scalar.copy(out=o, in_=i)
+
+        def q_x(G, ih):
+            nc.vector.quantize_mx(out=xc[:, G, 512 * ih:512 * (ih + 1)].bitcast(E4),
+                                  scales=xs[:, G, 512 * ih:512 * (ih + 1)], in_=ils[("x", G, ih)][:])
+
+        def il_d(G, a, eng):
+            il = ipool.tile([P, 1024], BF16, name="ild", tag="ild", align_bytes=64, bufs=3)
+            ils[("d", G, a)] = il
+            o = il[:].rearrange("p (n c j) -> p n c j", n=32, c=8)
+            i = dyns[G][:].rearrange("p j (n a c) -> p a n c j", a=4, c=8)[:, a]
+            if eng == "v":
+                nc.vector.tensor_copy(out=o, in_=i)
+            else:
+                nc.scalar.copy(out=o, in_=i)
+
+        def q_d(G, a):
+            nc.vector.quantize_mx(out=dyc[:, G, 256 * a:256 * (a + 1)].bitcast(E5),
+                                  scales=dys[:, G, 256 * a:256 * (a + 1)], in_=ils[("d", G, a)][:])
+
+        def pe_flip(s):
+            G, h = divmod(s, 2)
+            for g in range(2):
+                tp = ps.tile([P, 2, 2, P], F32, name="tp", tag="bank")
+                tps[(s, g)] = tp
+                for jj in range(2):
+                    words = dyns[G][:, 2 * h + jj, :].bitcast(F32)
+                    for u in range(2):
+                        nc.tensor.transpose(tp[:, jj, u, :], words[:, 256 * g + u:256 * (g + 1):2], ident[:])
+
+        def s_flip_out(s, g):
+            ti = tpool.tile([P, 1024], BF16, name="ti", tag="ti", align_bytes=64)
+            tis[(s, g)] = ti
+            nc.scalar.copy(out=ti[:].bitcast(F32).rearrange("p (j r u) -> p j r u", j=2, u=2),
+                           in_=tps[(s, g)][:].rearrange("p j u r -> p j r u"))
+
+        def q_t(s, g):
+            if g == 0:
+                tcd = cpool.tile([P, 2, 256], U32, name="tcd", tag="tcd", align_bytes=64)
+                tsc = cpool.tile([P, 2, 256], U8, name="tsc", tag="tsc", align_bytes=64)
+                tcds[s] = tcd
+                tscs[s] = tsc
+            nc.vector.quantize_mx(out=tcds[s][:, g, :].bitcast(E5), scales=tscs[s][:, g, :], in_=tis[(s, g)][:])
+
+        pxs, ots = {}, {}
+
+        def pe_dx(s, jj):
+            for ih in range(2):
+                px = ps.tile([P, 512], F32, name="px", tag="bank")
+                pxs[(s, jj, ih)] = px
+                for g in range(2):
+                    nc.tensor.matmul_mx(
+                        out=px[:],
+                        lhsT=tcds[s][:, g, P * jj:P * (jj + 1)].bitcast(E5),
+                        lhsT_scale=tscs[s][:, g, P * jj:P * (jj + 1)],
+                        rhs=wc[:, g, 512 * ih:512 * (ih + 1)].bitcast(E4),
+                        rhs_scale=ws[:, g, 512 * ih:512 * (ih + 1)],
+                        start=(g == 0), stop=(g == 1))
+
+        def dx_out(s, jj, ih, eng):
+            if ih == 0:
+                ot = opool.tile([P, IN_F], F32, name="ot", tag="ot")
+                ots[(s, jj)] = ot
+            o = ots[(s, jj)][:, 512 * ih:512 * (ih + 1)]
+            if eng == "v":
+                nc.vector.tensor_copy(out=o, in_=pxs[(s, jj, ih)][:])
+            else:
+                nc.scalar.copy(out=o, in_=pxs[(s, jj, ih)][:])
+            if ih == 1:
+                G, h = divmod(s, 2)
+                nc.sync.dma_start(out=o0_v[G, 2 * h + jj], in_=ots[(s, jj)][:])
+
+        pws, qts = {}, {}
+
+        def dw_alloc(a):
+            pool = ps2 if a % 2 == 0 else ps
+            for h in range(2):
+                for ih in range(2):
+                    pw = pool.tile([P, 512], F32, name="pw", tag="bank")
+                    pws[(a, h, ih)] = pw
+
+        def dw_pass(a, h, ih, G):
+            lo = 256 * a + P * h
+            nc.tensor.matmul_mx(
+                out=pws[(a, h, ih)][:],
+                lhsT=dyc[:, G, lo:lo + P].bitcast(E5),
+                lhsT_scale=dys[:, G, lo:lo + P],
+                rhs=xc[:, G, 512 * ih:512 * (ih + 1)].bitcast(E4),
+                rhs_scale=xs[:, G, 512 * ih:512 * (ih + 1)],
+                start=(G == 0), stop=(G == NG - 1))
+
+        def dw_out(a, h, ih, eng):
+            if ih == 0:
+                qt = opool.tile([P, IN_F], F32, name="ot", tag="ot")
+                qts[(a, h)] = qt
+            o = qts[(a, h)][:, 512 * ih:512 * (ih + 1)]
+            i = pws[(a, h, ih)][:]
+            if eng == "v":
+                if NEG[a]:
+                    nc.vector.tensor_scalar(out=o, in0=i, scalar1=-1.0, scalar2=None, op0=ALU.mult)
+                else:
+                    nc.vector.tensor_copy(out=o, in_=i)
+            elif NEG[a]:
+                nc.scalar.activation(out=o, in_=i, func=ACT.Copy, scale=-1.0)
+            else:
+                nc.scalar.copy(out=o, in_=i)
+            if ih == 1:
+                nc.sync.dma_start(out=o1_v[h, a], in_=qts[(a, h)][:])
+
+        NS = 8
+        items = [("x", 0, 0), ("x", 0, 1), ("w", 0, 0), ("w", 0, 1), ("w", 1, 0), ("w", 1, 1),
+                 ("x", 1, 0), ("x", 1, 1), ("x", 2, 0), ("x", 2, 1), ("x", 3, 0), ("x", 3, 1)]
+        plan = {-1: (0, 1), 0: (2, 3), 1: (4, 5), 2: (6,), 3: (7,), 4: (8,), 5: (9,), 6: (10,), 7: (11,)}
+        ENG = {}
+        load_x(0)
+        load_yg(0)
+        load_w(0)
+        load_w(1)
+        load_yg(1)
+        load_yg(2)
+        load_yg(3)
+        load_x(1)
+        late = {0: (("yg", 4),), 1: (("yg", 5), ("x", 2)), 2: (("yg", 6),), 3: (("yg", 7), ("x", 3))}
+        dw_alloc(0)
+
+        def il_item(it, eng):
+            if it[0] == "w":
+                il_w(it[1], it[2], eng)
+            else:
+                il_x(it[1], it[2], eng)
+
+        def q_item(it):
+            if it[0] == "w":
+                q_w(it[1], it[2])
+            else:
+                q_x(it[1], it[2])
+
+        for k in plan[-1]:
+            il_item(items[k], ENG.get(k, "v"))
+        for k in plan[-1]:
+            q_item(items[k])
+        LAGX = 2
+        for s in range(NS + LAGX + 1):
+            mine = plan.get(s, ())
+            if s < NS:
+                e_alloc(s)
+                v_turns(s)
+                s_tanh(s, 0)
+                s_tanh(s, 3)
+                v_relu(s)
+                v_reduce(s)
+                s_square(s, 0)
+                s_square(s, 3)
+                s_sin(s)
+            if 1 <= s <= NS:
+                pe_flip(s - 1)
+                s_flip_out(s - 1, 0)
+                s_flip_out(s - 1, 1)
+            for k in mine:
+                il_item(items[k], ENG.get(k, "v"))
+            if s < NS:
+                v_mul(s, 0)
+                v_mul(s, 3)
+            for k in mine:
+                q_item(items[k])
+            if s < NS:
+                v_mul(s, 1)
+            for what, n in late.get(s, ()):
+                if what == "yg":
+                    load_yg(n)
+                else:
+                    load_x(n)
+            if 1 <= s <= NS:
+                q_t(s - 1, 0)
+                q_t(s - 1, 1)
+            if 2 <= s <= NS and s % 2 == 0:
+                G = s // 2 - 1
+                il_d(G, 0, "v")
+            if LAGX <= s < NS + LAGX:
+                pe_dx(s - LAGX, 0)
+                pe_dx(s - LAGX, 1)
+                for jj in range(2):
+                    for ih in range(2):
+                        dx_out(s - LAGX, jj, ih, "s")
+            if 2 <= s <= NS and s % 2 == 0:
+                G = s // 2 - 1
+                q_d(G, 0)
+                for h in range(2):
+                    for ih in range(2):
+                        dw_pass(0, h, ih, G)
+        for h in range(2):
+            for ih in range(2):
+                dw_out(0, h, ih, "s")
+        for a in range(1, 4):
+            dw_alloc(a)
+            for G in range(NG):
+                il_d(G, a, "v")
+                q_d(G, a)
+                for h in range(2):
+                    for ih in range(2):
+                        dw_pass(a, h, ih, G)
+            for h in range(2):
+                for ih in range(2):
+                    dw_out(a, h, ih, "s" if (a < 3 or h == 0) else "v")

@@ -21,6 +21,74 @@ ALU = mybir.AluOpType
 P = 128
 NG = 4
 NEG = (True, False, False, True)
+GSLOT = {2: (0, 0), 0: (0, 1), 3: (1, 0), 1: (1, 1)}
+
+TASKS = (
+    ("lw", 0, 1, "a"), ("ly", 0), ("lg", 0), ("lg", 1), ("lw", 0, 0, "p"), ("lw", 1, 1, "a"), ("ly", 1), ("sh", 0, 0),
+    ("lw", 1, 0, "p"), ("pg", 0, 0), ("ly", 2), ("sh", 0, 3), ("lg", 2), ("vt", 0), ("vw", 0), ("vr", 0),
+    ("pg", 0, 1), ("lx", 1), ("sq", 0, 0), ("lx", 0), ("ss", 0), ("sq", 0, 3), ("vl", 0), ("ly", 3), ("vm", 0, 0),
+    ("vm", 0, 3), ("iw", 0, 0, "s"), ("iw", 0, 1, "v"), ("qw", 0, 0), ("sh", 1, 0), ("vm", 0, 1), ("lg", 4),
+    ("vt", 1), ("pf", 0, 0), ("vw", 1), ("pg", 1, 0), ("qw", 0, 1), ("sh", 1, 3), ("sq", 1, 3), ("sq", 1, 0),
+    ("fo", 0, 0, "s"), ("vr", 1), ("vl", 1), ("pf", 0, 1), ("ss", 1), ("lg", 3), ("vm", 1, 0), ("iw", 1, 1, "v"),
+    ("qt", 0, 0), ("pg", 1, 1), ("ly", 4), ("fo", 0, 1, "s"), ("iw", 1, 0, "s"), ("sh", 2, 0), ("lx", 2),
+    ("qt", 0, 1), ("qw", 1, 1), ("vm", 1, 3), ("qw", 1, 0), ("sq", 2, 0), ("ly", 5), ("vt", 2), ("pg", 2, 0),
+    ("px", 0, 0, 0), ("lg", 5), ("px", 0, 1, 0), ("vm", 1, 1), ("pf", 1, 0), ("pg", 2, 1), ("px", 0, 0, 1), ("lx", 3),
+    ("vw", 2), ("sh", 2, 3), ("xo", 0, 0, 0, "s"), ("pf", 1, 1), ("vl", 2), ("fo", 1, 0, "s"), ("vm", 2, 0),
+    ("fo", 1, 1, "s"), ("px", 0, 1, 1), ("qt", 1, 0), ("vr", 2), ("ix", 0, 0, "v"), ("xo", 0, 0, 1, "s"),
+    ("qt", 1, 1), ("sq", 2, 3), ("px", 1, 0, 0), ("px", 1, 0, 1), ("xo", 0, 1, 0, "v"), ("ss", 2), ("pg", 3, 0),
+    ("px", 1, 1, 0), ("xo", 0, 1, 1, "s"), ("sx", 0, 0), ("vm", 2, 3), ("sx", 0, 1), ("sh", 3, 0), ("ly", 6),
+    ("vm", 2, 1), ("qx", 0, 0), ("sh", 3, 3), ("pf", 2, 0), ("pf", 2, 1), ("fo", 2, 0, "s"), ("pg", 3, 1), ("vl", 3),
+    ("vt", 3), ("vw", 3), ("xo", 1, 0, 0, "v"), ("fo", 2, 1, "s"), ("qt", 2, 0), ("qt", 2, 1), ("sq", 3, 3),
+    ("vr", 3), ("sq", 3, 0), ("ss", 3), ("px", 1, 1, 1), ("vm", 3, 0), ("vm", 3, 3), ("xo", 1, 1, 0, "s"), ("vt", 4),
+    ("xo", 1, 0, 1, "s"), ("lg", 6), ("vm", 3, 1), ("px", 2, 0, 1), ("sh", 4, 0), ("sx", 1, 0), ("xo", 1, 1, 1, "s"),
+    ("pg", 4, 0), ("sx", 1, 1), ("ix", 1, 0, "v"), ("pf", 3, 0), ("pf", 3, 1), ("fo", 3, 0, "v"), ("px", 2, 0, 0),
+    ("vw", 4), ("pg", 4, 1), ("sh", 4, 3), ("fo", 3, 1, "s"), ("qx", 1, 0), ("vr", 4), ("vl", 4), ("sq", 4, 0),
+    ("px", 2, 1, 1), ("px", 2, 1, 0), ("qt", 3, 0), ("pg", 5, 0), ("sq", 4, 3), ("vm", 4, 0), ("ss", 4), ("sh", 5, 0),
+    ("qt", 3, 1), ("vm", 4, 3), ("xo", 2, 0, 1, "v"), ("vm", 4, 1), ("vt", 5), ("sh", 5, 3), ("pf", 4, 0), ("vl", 5),
+    ("xo", 2, 0, 0, "s"), ("ly", 7), ("sx", 2, 0), ("ix", 2, 0, "s"), ("pf", 4, 1), ("xo", 2, 1, 1, "s"), ("vw", 5),
+    ("lg", 7), ("fo", 4, 1, "s"), ("px", 3, 0, 0), ("xo", 2, 1, 0, "v"), ("vr", 5), ("qx", 2, 0), ("px", 3, 0, 1),
+    ("fo", 4, 0, "v"), ("px", 3, 1, 0), ("sq", 5, 0), ("sq", 5, 3), ("pg", 5, 1), ("qt", 4, 1), ("ss", 5),
+    ("vm", 5, 0), ("pg", 6, 0), ("xo", 3, 0, 1, "s"), ("xo", 3, 0, 0, "s"), ("sx", 2, 1), ("px", 3, 1, 1),
+    ("qt", 4, 0), ("px", 4, 0, 1), ("vt", 6), ("vl", 6), ("vm", 5, 3), ("xo", 3, 1, 1, "s"), ("vm", 5, 1),
+    ("xo", 3, 1, 0, "s"), ("px", 4, 1, 1), ("pf", 5, 0), ("pg", 6, 1), ("sh", 6, 0), ("vw", 6), ("pf", 5, 1),
+    ("ix", 3, 0, "v"), ("px", 4, 0, 0), ("vt", 7), ("qx", 3, 0), ("fo", 5, 0, "s"), ("sh", 6, 3), ("vr", 6),
+    ("sx", 3, 0), ("px", 4, 1, 0), ("fo", 5, 1, "s"), ("qt", 5, 1), ("sq", 6, 3), ("pg", 7, 0), ("qt", 5, 0),
+    ("sq", 6, 0), ("vm", 6, 0), ("ss", 6), ("vm", 6, 3), ("xo", 4, 0, 1, "s"), ("xo", 4, 1, 1, "s"), ("vm", 6, 1),
+    ("id", 0, 0, "v"), ("xo", 4, 0, 0, "s"), ("pf", 6, 1), ("sh", 7, 0), ("pf", 6, 0), ("sh", 7, 3), ("pg", 7, 1),
+    ("px", 5, 0, 0), ("vl", 7), ("id", 1, 0, "v"), ("sx", 3, 1), ("vw", 7), ("fo", 6, 0, "s"), ("id", 2, 0, "v"),
+    ("qd", 0, 0), ("fo", 6, 1, "s"), ("px", 5, 0, 1), ("vr", 7), ("xo", 5, 0, 1, "s"), ("qt", 6, 0), ("sq", 7, 0),
+    ("qd", 1, 0), ("qt", 6, 1), ("sx", 4, 0), ("id", 1, 1, "v"), ("px", 6, 0, 0), ("xo", 4, 1, 0, "s"),
+    ("px", 5, 1, 1), ("ss", 7), ("sx", 4, 1), ("sq", 7, 3), ("vm", 7, 0), ("vm", 7, 3), ("xo", 5, 0, 0, "s"),
+    ("px", 5, 1, 0), ("vm", 7, 1), ("pf", 7, 0), ("xo", 6, 0, 0, "s"), ("xo", 5, 1, 1, "s"), ("qd", 2, 0),
+    ("xo", 5, 1, 0, "s"), ("id", 3, 0, "v"), ("id", 0, 1, "v"), ("pf", 7, 1), ("px", 6, 1, 1), ("qd", 1, 1),
+    ("fo", 7, 0, "s"), ("px", 6, 0, 1), ("qd", 3, 0), ("fo", 7, 1, "s"), ("qt", 7, 1), ("px", 6, 1, 0),
+    ("xo", 6, 0, 1, "s"), ("qt", 7, 0), ("qd", 0, 1), ("id", 2, 1, "v"), ("sx", 5, 0), ("xo", 6, 1, 0, "s"),
+    ("px", 7, 0, 0), ("px", 7, 0, 1), ("qd", 2, 1), ("id", 0, 2, "v"), ("xo", 6, 1, 1, "s"), ("xo", 7, 0, 0, "s"),
+    ("sx", 5, 1), ("px", 7, 1, 0), ("sx", 6, 0), ("id", 3, 1, "s"), ("xo", 7, 0, 1, "s"), ("id", 1, 2, "v"),
+    ("xo", 7, 1, 0, "s"), ("px", 7, 1, 1), ("pw", 1, 0, 0, 0), ("sx", 7, 0), ("pw", 0, 0, 0, 0), ("pw", 0, 0, 0, 1),
+    ("xo", 7, 1, 1, "v"), ("qd", 3, 1), ("pw", 0, 1, 0, 0), ("pw", 0, 1, 0, 1), ("sx", 6, 1), ("qd", 0, 2),
+    ("pw", 0, 0, 0, 2), ("id", 2, 2, "v"), ("qd", 1, 2), ("qd", 2, 2), ("id", 3, 2, "s"), ("pw", 2, 1, 0, 0),
+    ("pw", 0, 1, 0, 2), ("pw", 0, 1, 0, 3), ("sx", 7, 1), ("pw", 0, 0, 0, 3), ("wo", 0, 1, 0, "s"),
+    ("pw", 1, 1, 0, 0), ("pw", 1, 0, 0, 1), ("id", 0, 3, "v"), ("id", 2, 3, "v"), ("pw", 1, 0, 0, 2),
+    ("pw", 1, 1, 0, 1), ("pw", 1, 1, 0, 2), ("pw", 1, 0, 0, 3), ("qd", 3, 2), ("wo", 1, 0, 0, "s"),
+    ("pw", 1, 1, 0, 3), ("pw", 2, 0, 0, 0), ("id", 1, 3, "v"), ("wo", 1, 1, 0, "s"), ("pw", 2, 0, 0, 1), ("qd", 1, 3),
+    ("pw", 2, 1, 0, 1), ("pw", 2, 1, 0, 2), ("sw", 1, 0, 0), ("pw", 2, 0, 0, 2), ("id", 3, 3, "s"),
+    ("pw", 2, 0, 0, 3), ("pw", 2, 1, 0, 3), ("qd", 0, 3), ("wo", 2, 0, 0, "s"), ("wo", 0, 0, 0, "s"), ("sw", 1, 1, 0),
+    ("pw", 3, 0, 0, 0), ("ix", 0, 1, "v"), ("pw", 3, 1, 0, 0), ("sw", 0, 1, 0), ("qd", 2, 3), ("sw", 0, 0, 0),
+    ("pw", 3, 1, 0, 1), ("pw", 3, 0, 0, 1), ("pw", 3, 0, 0, 2), ("pw", 3, 1, 0, 2), ("qd", 3, 3), ("sw", 2, 0, 0),
+    ("pw", 3, 0, 0, 3), ("pw", 3, 1, 0, 3), ("wo", 3, 0, 0, "s"), ("qx", 0, 1), ("ix", 1, 1, "v"),
+    ("wo", 3, 1, 0, "v"), ("pw", 3, 1, 1, 0), ("pw", 1, 1, 1, 0), ("sw", 3, 1, 0), ("pw", 0, 0, 1, 0),
+    ("wo", 2, 1, 0, "s"), ("pw", 1, 0, 1, 0), ("pw", 0, 1, 1, 0), ("pw", 2, 0, 1, 0), ("qx", 1, 1),
+    ("pw", 3, 1, 1, 1), ("sw", 2, 1, 0), ("pw", 3, 0, 1, 0), ("ix", 2, 1, "v"), ("pw", 0, 1, 1, 1), ("sw", 3, 0, 0),
+    ("pw", 0, 0, 1, 1), ("ix", 3, 1, "s"), ("qx", 2, 1), ("pw", 1, 0, 1, 1), ("pw", 3, 0, 1, 1), ("pw", 1, 1, 1, 1),
+    ("pw", 2, 1, 1, 0), ("pw", 2, 0, 1, 1), ("qx", 3, 1), ("pw", 0, 1, 1, 2), ("pw", 2, 1, 1, 1), ("pw", 2, 0, 1, 2),
+    ("pw", 2, 1, 1, 2), ("pw", 0, 0, 1, 2), ("pw", 1, 0, 1, 2), ("pw", 0, 0, 1, 3), ("pw", 3, 0, 1, 2),
+    ("pw", 0, 1, 1, 3), ("pw", 1, 1, 1, 2), ("wo", 0, 0, 1, "v"), ("pw", 3, 1, 1, 2), ("wo", 0, 1, 1, "s"),
+    ("sw", 0, 0, 1), ("sw", 0, 1, 1), ("pw", 1, 0, 1, 3), ("pw", 1, 1, 1, 3), ("wo", 1, 1, 1, "v"),
+    ("pw", 2, 0, 1, 3), ("pw", 2, 1, 1, 3), ("wo", 1, 0, 1, "s"), ("wo", 2, 0, 1, "v"), ("pw", 3, 0, 1, 3),
+    ("sw", 1, 0, 1), ("wo", 2, 1, 1, "v"), ("pw", 3, 1, 1, 3), ("sw", 1, 1, 1), ("sw", 2, 1, 1), ("wo", 3, 0, 1, "v"),
+    ("wo", 3, 1, 1, "s"), ("sw", 2, 0, 1), ("sw", 3, 0, 1), ("sw", 3, 1, 1),
+)
 
 
 def tile_vdl_v_kernel(tc, x_in, w_in, b_in, y_in, g_in, out_0, out_1):
@@ -36,17 +104,17 @@ def tile_vdl_v_kernel(tc, x_in, w_in, b_in, y_in, g_in, out_0, out_1):
         ctx.enter_context(tc.manual_schedule())
         const = ctx.enter_context(tc.tile_pool(name="const", bufs=1))
         keep = ctx.enter_context(tc.tile_pool(name="keep", bufs=1))
-        ypool = ctx.enter_context(tc.tile_pool(name="ypool", bufs=4))
-        gpool = ctx.enter_context(tc.tile_pool(name="gpool", bufs=4))
-        xpool = ctx.enter_context(tc.tile_pool(name="xpool", bufs=3))
+        ypool = ctx.enter_context(tc.tile_pool(name="ypool", bufs=3))
+        gpool = ctx.enter_context(tc.tile_pool(name="gpool", bufs=3))
+        xpool = ctx.enter_context(tc.tile_pool(name="xpool", bufs=4))
         epool = ctx.enter_context(tc.tile_pool(name="epool", bufs=2))
         dpool = ctx.enter_context(tc.tile_pool(name="dpool", bufs=4))
         ipool = ctx.enter_context(tc.tile_pool(name="ipool", bufs=3))
         tpool = ctx.enter_context(tc.tile_pool(name="tpool", bufs=4))
-        cpool = ctx.enter_context(tc.tile_pool(name="cpool", bufs=3))
-        opool = ctx.enter_context(tc.tile_pool(name="opool", bufs=6))
-        ps = ctx.enter_context(tc.psum_pool(name="ps_a", bufs=4))
-        ps2 = ctx.enter_context(tc.psum_pool(name="ps_b", bufs=4))
+        cpool = ctx.enter_context(tc.tile_pool(name="cpool", bufs=4))
+        opool = ctx.enter_context(tc.tile_pool(name="opool", bufs=4))
+        qpool = ctx.enter_context(tc.tile_pool(name="qpool", bufs=6))
+        ps = ctx.enter_context(tc.psum_pool(name="ps_all", bufs=8))
 
         warm = const.tile([P, 1], F32, name="warm")
         warm2 = const.tile([P, 1], F32, name="warm2")
@@ -54,6 +122,8 @@ def tile_vdl_v_kernel(tc, x_in, w_in, b_in, y_in, g_in, out_0, out_1):
         nc.scalar.activation(out=warm2[:], in_=warm[:], func=ACT.Silu)
         ident = const.tile([P, P], F32, name="ident")
         make_identity(nc, ident[:])
+        identb = const.tile([P, P], BF16, name="identb")
+        make_identity(nc, identb[:])
         pidx = const.tile([P, 1], I32, name="pidx")
         nc.gpsimd.iota(pidx[:], pattern=[[0, 1]], base=2, channel_multiplier=1)
         pbit = const.tile([P, 1], I32, name="pbit")
@@ -69,28 +139,33 @@ def tile_vdl_v_kernel(tc, x_in, w_in, b_in, y_in, g_in, out_0, out_1):
         wc = keep.tile([P, 2, IN_F], U32, name="wc", align_bytes=64)
         ws = keep.tile([P, 2, IN_F], U8, name="ws", align_bytes=64)
 
-        yts, gts, xts, wts, dyns, tcds, tscs, ets, tps, tis, ils = {}, {}, {}, {}, {}, {}, {}, {}, {}, {}, {}
+        held = {}
 
-        def load_yg(s):
+        def load_y(s):
             G, h = divmod(s, 2)
             yt = ypool.tile([P, 2, OUT_F], F32, name="yt", tag="yt")
             nc.sync.dma_start(out=yt[:], in_=y_v[G][:, 2 * h:2 * h + 2, :])
+            held[("y", s)] = yt[:].rearrange("p j w -> p (j w)")
+
+        def load_g(s):
+            G, h = divmod(s, 2)
             gt = gpool.tile([P, 2, OUT_F], BF16, name="gt", tag="gt")
             nc.sync.dma_start(out=gt[:], in_=g_v[G][:, 2 * h:2 * h + 2, :])
-            yts[s] = yt[:].rearrange("p j w -> p (j w)")
-            gts[s] = gt[:].rearrange("p j w -> p (j w)")
+            held[("g", s)] = gt[:].rearrange("p j w -> p (j w)")
 
         def load_x(G):
             xt = xpool.tile([P, 4, IN_F], BF16, name="xt", tag="xw")
             nc.sync.dma_start(out=xt[:], in_=x_v[G])
-            xts[G] = xt
+            held[("x", G)] = xt
 
-        def load_w(g):
-            wt = xpool.tile([P, 4, IN_F], BF16, name="wt", tag="xw")
-            for a in range(4):
+        def load_w(g, half, queue):
+            if ("w", g) not in held:
+                wt = xpool.tile([P, 4, IN_F], BF16, name="wt", tag="xw")
+                held[("w", g)] = wt
+            for a in (2 * half, 2 * half + 1):
                 for c2 in range(2):
-                    nc.sync.dma_start(out=wt[2 * a + c2:P:8, :, :], in_=w_v[g, c2, a])
-            wts[g] = wt
+                    (nc.sync if queue == "p" else nc.scalar).dma_start(out=held[("w", g)][2 * a + c2:P:8, :, :],
+                                                                       in_=w_v[g, c2, a])
 
         def col(flat, a):
             return flat[:, a:2048:4]
@@ -98,57 +173,81 @@ def tile_vdl_v_kernel(tc, x_in, w_in, b_in, y_in, g_in, out_0, out_1):
         def runs(ap):
             return ap.rearrange("p (n c) -> p n c", c=8)
 
+        def dyn(G):
+            if ("dyn", G) not in held:
+                t = dpool.tile([P, 4, OUT_F], BF16, name="dyn", tag="dyn", align_bytes=64)
+                held[("dyn", G)] = t
+            return held[("dyn", G)]
+
         def dst(s, a):
             G, h = divmod(s, 2)
-            return dyns[G][:].rearrange("p j w -> p (j w)")[:, 2048 * h:2048 * (h + 1)].rearrange(
+            return dyn(G)[:].rearrange("p j w -> p (j w)")[:, 2048 * h:2048 * (h + 1)].rearrange(
                 "p (n a c) -> p a n c", a=4, c=8)[:, a]
 
-        def e_alloc(s):
-            if s % 2 == 0:
-                dyn = dpool.tile([P, 4, OUT_F], BF16, name="dyn", tag="dyn", align_bytes=64)
-                dyns[s // 2] = dyn
-            t0 = epool.tile([P, 512], F32, name="t0", tag="t0")
-            t3 = epool.tile([P, 512], F32, name="t3", tag="t3")
-            kk = epool.tile([P, 512], I32, name="kk", tag="kk")
-            rr = epool.tile([P, 512], F32, name="rr", tag="rr")
-            ets[s] = (t0, t3, kk, rr)
+        def work(kind, s, dtype):
+            if (kind, s) not in held:
+                t = epool.tile([P, 512], dtype, name=kind, tag=kind)
+                held[(kind, s)] = t
+            return held[(kind, s)]
+
+        def pe_g(s, k):
+            gp = ps.tile([P, 2, 512], BF16, name="gp", tag="bank")
+            held[("gp", s, k)] = gp
+            for a in range(4):
+                if GSLOT[a][0] == k:
+                    nc.tensor.matmul(out=gp[:, GSLOT[a][1], :], lhsT=identb[:], rhs=col(held[("g", s)], a),
+                                     start=True, stop=True)
+
+        def gcol(s, a):
+            k, i = GSLOT[a]
+            return runs(held[("gp", s, k)][:, i, :])
 
         def v_turns(s):
-            nc.vector.tensor_scalar(out=ets[s][2][:], in0=col(yts[s], 1), scalar1=1.0 / (2.0 * math.pi), scalar2=0.25,
-                                    op0=ALU.mult, op1=ALU.add)
+            nc.vector.tensor_scalar(out=work("rr", s, F32)[:], in0=col(held[("y", s)], 1), scalar1=1.0 / (2.0 * math.pi),
+                                    scalar2=0.25, op0=ALU.mult, op1=ALU.add)
+
+        def v_whole(s):
+            nc.vector.tensor_copy(out=work("kk", s, I32)[:], in_=work("rr", s, F32)[:])
 
         def v_reduce(s):
-            nc.vector.scalar_tensor_tensor(out=ets[s][3][:], in0=ets[s][2][:], scalar=-2.0 * math.pi, in1=col(yts[s], 1),
-                                           op0=ALU.mult, op1=ALU.add)
+            nc.vector.scalar_tensor_tensor(out=work("rr", s, F32)[:], in0=work("kk", s, I32)[:], scalar=-1.0,
+                                           in1=work("rr", s, F32)[:], op0=ALU.mult, op1=ALU.add)
 
         def v_relu(s):
-            nc.vector.scalar_tensor_tensor(out=dst(s, 2), in0=runs(col(yts[s], 2)), scalar=0.0, in1=runs(col(gts[s], 2)),
+            nc.vector.scalar_tensor_tensor(out=dst(s, 2), in0=runs(col(held[("y", s)], 2)), scalar=0.0, in1=gcol(s, 2),
                                            op0=ALU.is_gt, op1=ALU.mult)
 
         def s_tanh(s, a):
-            nc.scalar.activation(out=ets[s][0 if a == 0 else 1][:], in_=col(yts[s], a), func=ACT.Tanh,
+            nc.scalar.activation(out=work("t%d" % a, s, F32)[:], in_=col(held[("y", s)], a), func=ACT.Tanh,
                                  scale=1.0 if a == 0 else 0.5)
 
         def s_square(s, a):
-            t = ets[s][0 if a == 0 else 1]
+            t = work("t%d" % a, s, F32)
             nc.scalar.activation(out=t[:], in_=t[:], func=ACT.Square, scale=1.0 if a == 0 else 0.5)
 
         def s_sin(s):
-            nc.scalar.activation(out=ets[s][3][:], in_=ets[s][3][:], func=ACT.Sin, bias=0.5 * math.pi)
+            t = work("rr", s, F32)
+            nc.scalar.activation(out=t[:], in_=t[:], func=ACT.Sin, scale=2.0 * math.pi)
 
         def v_mul(s, a):
             if a == 1:
-                nc.vector.tensor_tensor(out=dst(s, 1), in0=runs(ets[s][3][:]), in1=runs(col(gts[s], 1)), op=ALU.mult)
+                nc.vector.tensor_tensor(out=dst(s, 1), in0=runs(work("rr", s, F32)[:]), in1=gcol(s, 1), op=ALU.mult)
             else:
-                nc.vector.scalar_tensor_tensor(out=dst(s, a), in0=runs(ets[s][0 if a == 0 else 1][:]),
-                                               scalar=1.0 if a == 0 else 0.25, in1=runs(col(gts[s], a)),
+                nc.vector.scalar_tensor_tensor(out=dst(s, a), in0=runs(work("t%d" % a, s, F32)[:]),
+                                               scalar=1.0 if a == 0 else 0.25, in1=gcol(s, a),
                                                op0=ALU.subtract, op1=ALU.mult)
+
+        def copy_on(eng, o, i):
+            if eng == "v":
+                nc.vector.tensor_copy(out=o, in_=i)
+            else:
+                nc.scalar.copy(out=o, in_=i)
 
         def il_w(g, ih, eng):
             il = ipool.tile([P, 2048], BF16, name="il", tag="il", align_bytes=64)
-            ils[("w", g, ih)] = il
-            o = il[:].rearrange("p (i t) -> p i t", t=4)
-            i = wts[g][:, :, 512 * ih:512 * (ih + 1)].rearrange("p t i -> p i t")
+            held[("ilw", g, ih)] = il
+            o = il[:].rearrange("p (c i t) -> p c t i", i=4, t=4)
+            i = held[("w", g)][:, :, 512 * ih:512 * (ih + 1)].rearrange("p t (c i) -> p c t i", i=4)
             if eng == "v":
                 nc.vector.tensor_scalar(out=o, in0=i, scalar1=sgn[:, 0:1], scalar2=None, op0=ALU.mult)
             else:
@@ -156,101 +255,86 @@ def tile_vdl_v_kernel(tc, x_in, w_in, b_in, y_in, g_in, out_0, out_1):
 
         def q_w(g, ih):
             nc.vector.quantize_mx(out=wc[:, g, 512 * ih:512 * (ih + 1)].bitcast(E4),
-                                  scales=ws[:, g, 512 * ih:512 * (ih + 1)], in_=ils[("w", g, ih)][:])
+                                  scales=ws[:, g, 512 * ih:512 * (ih + 1)], in_=held[("ilw", g, ih)][:])
 
         def il_x(G, ih, eng):
             il = ipool.tile([P, 2048], BF16, name="il", tag="il", align_bytes=64)
-            ils[("x", G, ih)] = il
-            o = il[:].rearrange("p (i j) -> p i j", j=4)
-            i = xts[G][:, :, 512 * ih:512 * (ih + 1)].rearrange("p j i -> p i j")
-            if eng == "v":
-                nc.vector.tensor_copy(out=o, in_=i)
-            else:
-                nc.scalar.copy(out=o, in_=i)
+            held[("ilx", G, ih)] = il
+            copy_on(eng, il[:].rearrange("p (c i j) -> p c j i", i=4, j=4),
+                    held[("x", G)][:, :, 512 * ih:512 * (ih + 1)].rearrange("p j (c i) -> p c j i", i=4))
 
         def q_x(G, ih):
             nc.vector.quantize_mx(out=xc[:, G, 512 * ih:512 * (ih + 1)].bitcast(E4),
-                                  scales=xs[:, G, 512 * ih:512 * (ih + 1)], in_=ils[("x", G, ih)][:])
+                                  scales=xs[:, G, 512 * ih:512 * (ih + 1)], in_=held[("ilx", G, ih)][:])
 
         def il_d(G, a, eng):
-            il = ipool.tile([P, 1024], BF16, name="ild", tag="ild", align_bytes=64, bufs=3)
-            ils[("d", G, a)] = il
-            o = il[:].rearrange("p (n c j) -> p n c j", n=32, c=8)
-            i = dyns[G][:].rearrange("p j (n a c) -> p a n c j", a=4, c=8)[:, a]
+            il = ipool.tile([P, 1024], BF16, name="ild", tag="ild", align_bytes=64)
+            held[("ild", G, a)] = il
+            o = il[:].rearrange("p (n c i j) -> p n c j i", n=32, c=2, i=4)
+            i = dyn(G)[:].rearrange("p j (n a c i) -> p a n c j i", a=4, c=2, i=4)[:, a]
             if eng == "v":
                 nc.vector.tensor_copy(out=o, in_=i)
             else:
-                nc.scalar.copy(out=o, in_=i)
+                for c in range(2):
+                    nc.scalar.copy(out=o[:, :, c], in_=i[:, :, c])
 
         def q_d(G, a):
             nc.vector.quantize_mx(out=dyc[:, G, 256 * a:256 * (a + 1)].bitcast(E5),
-                                  scales=dys[:, G, 256 * a:256 * (a + 1)], in_=ils[("d", G, a)][:])
+                                  scales=dys[:, G, 256 * a:256 * (a + 1)], in_=held[("ild", G, a)][:])
 
-        def pe_flip(s):
+        def pe_flip(s, g):
             G, h = divmod(s, 2)
-            for g in range(2):
-                tp = ps.tile([P, 2, 2, P], F32, name="tp", tag="bank")
-                tps[(s, g)] = tp
-                for jj in range(2):
-                    words = dyns[G][:, 2 * h + jj, :].bitcast(F32)
-                    for u in range(2):
-                        nc.tensor.transpose(tp[:, jj, u, :], words[:, 256 * g + u:256 * (g + 1):2], ident[:])
+            tp = ps.tile([P, 2, 2, P], F32, name="tp", tag="bank")
+            held[("tp", s, g)] = tp
+            for jj in range(2):
+                words = dyn(G)[:, 2 * h + jj, :].bitcast(F32)
+                for u in range(2):
+                    nc.tensor.transpose(tp[:, jj, u, :], words[:, 256 * g + u:256 * (g + 1):2], ident[:])
 
-        def s_flip_out(s, g):
+        def flip_out(s, g, eng):
             ti = tpool.tile([P, 1024], BF16, name="ti", tag="ti", align_bytes=64)
-            tis[(s, g)] = ti
-            nc.scalar.copy(out=ti[:].bitcast(F32).rearrange("p (j r u) -> p j r u", j=2, u=2),
-                           in_=tps[(s, g)][:].rearrange("p j u r -> p j r u"))
+            held[("ti", s, g)] = ti
+            copy_on(eng, ti[:].bitcast(F32).rearrange("p (j r u) -> p j r u", j=2, u=2),
+                    held[("tp", s, g)][:].rearrange("p j u r -> p j r u"))
 
         def q_t(s, g):
-            if g == 0:
+            if ("tcd", s) not in held:
                 tcd = cpool.tile([P, 2, 256], U32, name="tcd", tag="tcd", align_bytes=64)
                 tsc = cpool.tile([P, 2, 256], U8, name="tsc", tag="tsc", align_bytes=64)
-                tcds[s] = tcd
-                tscs[s] = tsc
-            nc.vector.quantize_mx(out=tcds[s][:, g, :].bitcast(E5), scales=tscs[s][:, g, :], in_=tis[(s, g)][:])
+                held[("tcd", s)] = tcd
+                held[("tsc", s)] = tsc
+            nc.vector.quantize_mx(out=held[("tcd", s)][:, g, :].bitcast(E5), scales=held[("tsc", s)][:, g, :],
+                                  in_=held[("ti", s, g)][:])
 
-        pxs, ots = {}, {}
-
-        def pe_dx(s, jj):
-            for ih in range(2):
-                px = ps.tile([P, 512], F32, name="px", tag="bank")
-                pxs[(s, jj, ih)] = px
-                for g in range(2):
-                    nc.tensor.matmul_mx(
-                        out=px[:],
-                        lhsT=tcds[s][:, g, P * jj:P * (jj + 1)].bitcast(E5),
-                        lhsT_scale=tscs[s][:, g, P * jj:P * (jj + 1)],
-                        rhs=wc[:, g, 512 * ih:512 * (ih + 1)].bitcast(E4),
-                        rhs_scale=ws[:, g, 512 * ih:512 * (ih + 1)],
-                        start=(g == 0), stop=(g == 1))
+        def pe_dx(s, jj, ih):
+            px = ps.tile([P, 512], F32, name="px", tag="bank")
+            held[("px", s, jj, ih)] = px
+            for g in range(2):
+                nc.tensor.matmul_mx(
+                    out=px[:],
+                    lhsT=held[("tcd", s)][:, g, P * jj:P * (jj + 1)].bitcast(E5),
+                    lhsT_scale=held[("tsc", s)][:, g, P * jj:P * (jj + 1)],
+                    rhs=wc[:, g, 512 * ih:512 * (ih + 1)].bitcast(E4),
+                    rhs_scale=ws[:, g, 512 * ih:512 * (ih + 1)],
+                    start=(g == 0), stop=(g == 1))
 
         def dx_out(s, jj, ih, eng):
-            if ih == 0:
+            if ("ot", s, jj) not in held:
                 ot = opool.tile([P, IN_F], F32, name="ot", tag="ot")
-                ots[(s, jj)] = ot
-            o = ots[(s, jj)][:, 512 * ih:512 * (ih + 1)]
-            if eng == "v":
-                nc.vector.tensor_copy(out=o, in_=pxs[(s, jj, ih)][:])
-            else:
-                nc.scalar.copy(out=o, in_=pxs[(s, jj, ih)][:])
-            if ih == 1:
-                G, h = divmod(s, 2)
-                nc.sync.dma_start(out=o0_v[G, 2 * h + jj], in_=ots[(s, jj)][:])
+                held[("ot", s, jj)] = ot
+            copy_on(eng, held[("ot", s, jj)][:, 512 * ih:512 * (ih + 1)], held[("px", s, jj, ih)][:])
 
-        pws, qts = {}, {}
-
-        def dw_alloc(a):
-            pool = ps2 if a % 2 == 0 else ps
-            for h in range(2):
-                for ih in range(2):
-                    pw = pool.tile([P, 512], F32, name="pw", tag="bank")
-                    pws[(a, h, ih)] = pw
+        def st_dx(s, jj):
+            G, h = divmod(s, 2)
+            nc.sync.dma_start(out=o0_v[G, 2 * h + jj], in_=held[("ot", s, jj)][:])
 
         def dw_pass(a, h, ih, G):
+            if ("pw", a, h, ih) not in held:
+                pw = ps.tile([P, 512], F32, name="pw", tag="bank")
+                held[("pw", a, h, ih)] = pw
             lo = 256 * a + P * h
             nc.tensor.matmul_mx(
-                out=pws[(a, h, ih)][:],
+                out=held[("pw", a, h, ih)][:],
                 lhsT=dyc[:, G, lo:lo + P].bitcast(E5),
                 lhsT_scale=dys[:, G, lo:lo + P],
                 rhs=xc[:, G, 512 * ih:512 * (ih + 1)].bitcast(E4),
@@ -258,115 +342,22 @@ def tile_vdl_v_kernel(tc, x_in, w_in, b_in, y_in, g_in, out_0, out_1):
                 start=(G == 0), stop=(G == NG - 1))
 
         def dw_out(a, h, ih, eng):
-            if ih == 0:
-                qt = opool.tile([P, IN_F], F32, name="ot", tag="ot")
-                qts[(a, h)] = qt
-            o = qts[(a, h)][:, 512 * ih:512 * (ih + 1)]
-            i = pws[(a, h, ih)][:]
-            if eng == "v":
-                if NEG[a]:
-                    nc.vector.tensor_scalar(out=o, in0=i, scalar1=-1.0, scalar2=None, op0=ALU.mult)
-                else:
-                    nc.vector.tensor_copy(out=o, in_=i)
-            elif NEG[a]:
-                nc.scalar.activation(out=o, in_=i, func=ACT.Copy, scale=-1.0)
+            qt = qpool.tile([P, 512], F32, name="qt", tag="qt")
+            held[("qt", a, h, ih)] = qt
+            i = held[("pw", a, h, ih)][:]
+            if not NEG[a]:
+                copy_on(eng, qt[:], i)
+            elif eng == "v":
+                nc.vector.tensor_scalar(out=qt[:], in0=i, scalar1=-1.0, scalar2=None, op0=ALU.mult)
             else:
-                nc.scalar.copy(out=o, in_=i)
-            if ih == 1:
-                nc.sync.dma_start(out=o1_v[h, a], in_=qts[(a, h)][:])
+                nc.scalar.activation(out=qt[:], in_=i, func=ACT.Copy, scale=-1.0)
 
-        NS = 8
-        items = [("x", 0, 0), ("x", 0, 1), ("w", 0, 0), ("w", 0, 1), ("w", 1, 0), ("w", 1, 1),
-                 ("x", 1, 0), ("x", 1, 1), ("x", 2, 0), ("x", 2, 1), ("x", 3, 0), ("x", 3, 1)]
-        plan = {-1: (0, 1), 0: (2, 3), 1: (4, 5), 2: (6,), 3: (7,), 4: (8,), 5: (9,), 6: (10,), 7: (11,)}
-        ENG = {}
-        load_x(0)
-        load_yg(0)
-        load_w(0)
-        load_w(1)
-        load_yg(1)
-        load_yg(2)
-        load_yg(3)
-        load_x(1)
-        late = {0: (("yg", 4),), 1: (("yg", 5), ("x", 2)), 2: (("yg", 6),), 3: (("yg", 7), ("x", 3))}
-        dw_alloc(0)
+        def st_dw(a, h, ih):
+            nc.sync.dma_start(out=o1_v[h, a][:, 512 * ih:512 * (ih + 1)], in_=held[("qt", a, h, ih)][:])
 
-        def il_item(it, eng):
-            if it[0] == "w":
-                il_w(it[1], it[2], eng)
-            else:
-                il_x(it[1], it[2], eng)
-
-        def q_item(it):
-            if it[0] == "w":
-                q_w(it[1], it[2])
-            else:
-                q_x(it[1], it[2])
-
-        for k in plan[-1]:
-            il_item(items[k], ENG.get(k, "v"))
-        for k in plan[-1]:
-            q_item(items[k])
-        LAGX = 2
-        for s in range(NS + LAGX + 1):
-            mine = plan.get(s, ())
-            if s < NS:
-                e_alloc(s)
-                v_turns(s)
-                s_tanh(s, 0)
-                s_tanh(s, 3)
-                v_relu(s)
-                v_reduce(s)
-                s_square(s, 0)
-                s_square(s, 3)
-                s_sin(s)
-            if 1 <= s <= NS:
-                pe_flip(s - 1)
-                s_flip_out(s - 1, 0)
-                s_flip_out(s - 1, 1)
-            for k in mine:
-                il_item(items[k], ENG.get(k, "v"))
-            if s < NS:
-                v_mul(s, 0)
-                v_mul(s, 3)
-            for k in mine:
-                q_item(items[k])
-            if s < NS:
-                v_mul(s, 1)
-            for what, n in late.get(s, ()):
-                if what == "yg":
-                    load_yg(n)
-                else:
-                    load_x(n)
-            if 1 <= s <= NS:
-                q_t(s - 1, 0)
-                q_t(s - 1, 1)
-            if 2 <= s <= NS and s % 2 == 0:
-                G = s // 2 - 1
-                il_d(G, 0, "v")
-            if LAGX <= s < NS + LAGX:
-                pe_dx(s - LAGX, 0)
-                pe_dx(s - LAGX, 1)
-                for jj in range(2):
-                    for ih in range(2):
-                        dx_out(s - LAGX, jj, ih, "s")
-            if 2 <= s <= NS and s % 2 == 0:
-                G = s // 2 - 1
-                q_d(G, 0)
-                for h in range(2):
-                    for ih in range(2):
-                        dw_pass(0, h, ih, G)
-        for h in range(2):
-            for ih in range(2):
-                dw_out(0, h, ih, "s")
-        for a in range(1, 4):
-            dw_alloc(a)
-            for G in range(NG):
-                il_d(G, a, "v")
-                q_d(G, a)
-                for h in range(2):
-                    for ih in range(2):
-                        dw_pass(a, h, ih, G)
-            for h in range(2):
-                for ih in range(2):
-                    dw_out(a, h, ih, "s" if (a < 3 or h == 0) else "v")
+        fns = {"ly": load_y, "lg": load_g, "lx": load_x, "lw": load_w, "pg": pe_g, "vt": v_turns, "vw": v_whole,
+               "vr": v_reduce, "vl": v_relu, "sh": s_tanh, "sq": s_square, "ss": s_sin, "vm": v_mul,
+               "iw": il_w, "qw": q_w, "ix": il_x, "qx": q_x, "id": il_d, "qd": q_d, "pf": pe_flip, "fo": flip_out,
+               "qt": q_t, "px": pe_dx, "xo": dx_out, "sx": st_dx, "pw": dw_pass, "wo": dw_out, "sw": st_dw}
+        for t in TASKS:
+            fns[t[0]](*t[1:])

@@ -13,82 +13,20 @@ BF16 = mybir.dt.bfloat16
 I32 = mybir.dt.int32
 U32 = mybir.dt.uint32
 U8 = mybir.dt.uint8
-E4 = mybir.dt.float8_e4m3fn_x4
-E5 = mybir.dt.float8_e5m2_x4
+E4M3 = mybir.dt.float8_e4m3fn_x4
+E5M2 = mybir.dt.float8_e5m2_x4
 ACT = mybir.ActivationFunctionType
 ALU = mybir.AluOpType
 
 P = 128
-NG = 4
-NEG = (True, False, False, True)
-GSLOT = {2: (0, 0), 0: (0, 1), 3: (1, 0), 1: (1, 1)}
-
-TASKS = (
-    ("lw", 0, 1, "a"), ("ly", 0), ("lg", 0), ("lg", 1), ("lw", 0, 0, "p"), ("lw", 1, 1, "a"), ("ly", 1), ("sh", 0, 0),
-    ("lw", 1, 0, "p"), ("pg", 0, 0), ("ly", 2), ("sh", 0, 3), ("lg", 2), ("vt", 0), ("vw", 0), ("vr", 0),
-    ("pg", 0, 1), ("lx", 1), ("sq", 0, 0), ("lx", 0), ("ss", 0), ("sq", 0, 3), ("vl", 0), ("ly", 3), ("vm", 0, 0),
-    ("vm", 0, 3), ("iw", 0, 0, "s"), ("iw", 0, 1, "v"), ("qw", 0, 0), ("sh", 1, 0), ("vm", 0, 1), ("lg", 4),
-    ("vt", 1), ("pf", 0, 0), ("vw", 1), ("pg", 1, 0), ("qw", 0, 1), ("sh", 1, 3), ("sq", 1, 3), ("sq", 1, 0),
-    ("fo", 0, 0, "s"), ("vr", 1), ("vl", 1), ("pf", 0, 1), ("ss", 1), ("lg", 3), ("vm", 1, 0), ("iw", 1, 1, "v"),
-    ("qt", 0, 0), ("pg", 1, 1), ("ly", 4), ("fo", 0, 1, "s"), ("iw", 1, 0, "s"), ("sh", 2, 0), ("lx", 2),
-    ("qt", 0, 1), ("qw", 1, 1), ("vm", 1, 3), ("qw", 1, 0), ("sq", 2, 0), ("ly", 5), ("vt", 2), ("pg", 2, 0),
-    ("px", 0, 0, 0), ("lg", 5), ("px", 0, 1, 0), ("vm", 1, 1), ("pf", 1, 0), ("pg", 2, 1), ("px", 0, 0, 1), ("lx", 3),
-    ("vw", 2), ("sh", 2, 3), ("xo", 0, 0, 0, "s"), ("pf", 1, 1), ("vl", 2), ("fo", 1, 0, "s"), ("vm", 2, 0),
-    ("fo", 1, 1, "s"), ("px", 0, 1, 1), ("qt", 1, 0), ("vr", 2), ("ix", 0, 0, "v"), ("xo", 0, 0, 1, "s"),
-    ("qt", 1, 1), ("sq", 2, 3), ("px", 1, 0, 0), ("px", 1, 0, 1), ("xo", 0, 1, 0, "v"), ("ss", 2), ("pg", 3, 0),
-    ("px", 1, 1, 0), ("xo", 0, 1, 1, "s"), ("sx", 0, 0), ("vm", 2, 3), ("sx", 0, 1), ("sh", 3, 0), ("ly", 6),
-    ("vm", 2, 1), ("qx", 0, 0), ("sh", 3, 3), ("pf", 2, 0), ("pf", 2, 1), ("fo", 2, 0, "s"), ("pg", 3, 1), ("vl", 3),
-    ("vt", 3), ("vw", 3), ("xo", 1, 0, 0, "v"), ("fo", 2, 1, "s"), ("qt", 2, 0), ("qt", 2, 1), ("sq", 3, 3),
-    ("vr", 3), ("sq", 3, 0), ("ss", 3), ("px", 1, 1, 1), ("vm", 3, 0), ("vm", 3, 3), ("xo", 1, 1, 0, "s"), ("vt", 4),
-    ("xo", 1, 0, 1, "s"), ("lg", 6), ("vm", 3, 1), ("px", 2, 0, 1), ("sh", 4, 0), ("sx", 1, 0), ("xo", 1, 1, 1, "s"),
-    ("pg", 4, 0), ("sx", 1, 1), ("ix", 1, 0, "v"), ("pf", 3, 0), ("pf", 3, 1), ("fo", 3, 0, "v"), ("px", 2, 0, 0),
-    ("vw", 4), ("pg", 4, 1), ("sh", 4, 3), ("fo", 3, 1, "s"), ("qx", 1, 0), ("vr", 4), ("vl", 4), ("sq", 4, 0),
-    ("px", 2, 1, 1), ("px", 2, 1, 0), ("qt", 3, 0), ("pg", 5, 0), ("sq", 4, 3), ("vm", 4, 0), ("ss", 4), ("sh", 5, 0),
-    ("qt", 3, 1), ("vm", 4, 3), ("xo", 2, 0, 1, "v"), ("vm", 4, 1), ("vt", 5), ("sh", 5, 3), ("pf", 4, 0), ("vl", 5),
-    ("xo", 2, 0, 0, "s"), ("ly", 7), ("sx", 2, 0), ("ix", 2, 0, "s"), ("pf", 4, 1), ("xo", 2, 1, 1, "s"), ("vw", 5),
-    ("lg", 7), ("fo", 4, 1, "s"), ("px", 3, 0, 0), ("xo", 2, 1, 0, "v"), ("vr", 5), ("qx", 2, 0), ("px", 3, 0, 1),
-    ("fo", 4, 0, "v"), ("px", 3, 1, 0), ("sq", 5, 0), ("sq", 5, 3), ("pg", 5, 1), ("qt", 4, 1), ("ss", 5),
-    ("vm", 5, 0), ("pg", 6, 0), ("xo", 3, 0, 1, "s"), ("xo", 3, 0, 0, "s"), ("sx", 2, 1), ("px", 3, 1, 1),
-    ("qt", 4, 0), ("px", 4, 0, 1), ("vt", 6), ("vl", 6), ("vm", 5, 3), ("xo", 3, 1, 1, "s"), ("vm", 5, 1),
-    ("xo", 3, 1, 0, "s"), ("px", 4, 1, 1), ("pf", 5, 0), ("pg", 6, 1), ("sh", 6, 0), ("vw", 6), ("pf", 5, 1),
-    ("ix", 3, 0, "v"), ("px", 4, 0, 0), ("vt", 7), ("qx", 3, 0), ("fo", 5, 0, "s"), ("sh", 6, 3), ("vr", 6),
-    ("sx", 3, 0), ("px", 4, 1, 0), ("fo", 5, 1, "s"), ("qt", 5, 1), ("sq", 6, 3), ("pg", 7, 0), ("qt", 5, 0),
-    ("sq", 6, 0), ("vm", 6, 0), ("ss", 6), ("vm", 6, 3), ("xo", 4, 0, 1, "s"), ("xo", 4, 1, 1, "s"), ("vm", 6, 1),
-    ("id", 0, 0, "v"), ("xo", 4, 0, 0, "s"), ("pf", 6, 1), ("sh", 7, 0), ("pf", 6, 0), ("sh", 7, 3), ("pg", 7, 1),
-    ("px", 5, 0, 0), ("vl", 7), ("id", 1, 0, "v"), ("sx", 3, 1), ("vw", 7), ("fo", 6, 0, "s"), ("id", 2, 0, "v"),
-    ("qd", 0, 0), ("fo", 6, 1, "s"), ("px", 5, 0, 1), ("vr", 7), ("xo", 5, 0, 1, "s"), ("qt", 6, 0), ("sq", 7, 0),
-    ("qd", 1, 0), ("qt", 6, 1), ("sx", 4, 0), ("id", 1, 1, "v"), ("px", 6, 0, 0), ("xo", 4, 1, 0, "s"),
-    ("px", 5, 1, 1), ("ss", 7), ("sx", 4, 1), ("sq", 7, 3), ("vm", 7, 0), ("vm", 7, 3), ("xo", 5, 0, 0, "s"),
-    ("px", 5, 1, 0), ("vm", 7, 1), ("pf", 7, 0), ("xo", 6, 0, 0, "s"), ("xo", 5, 1, 1, "s"), ("qd", 2, 0),
-    ("xo", 5, 1, 0, "s"), ("id", 3, 0, "v"), ("id", 0, 1, "v"), ("pf", 7, 1), ("px", 6, 1, 1), ("qd", 1, 1),
-    ("fo", 7, 0, "s"), ("px", 6, 0, 1), ("qd", 3, 0), ("fo", 7, 1, "s"), ("qt", 7, 1), ("px", 6, 1, 0),
-    ("xo", 6, 0, 1, "s"), ("qt", 7, 0), ("qd", 0, 1), ("id", 2, 1, "v"), ("sx", 5, 0), ("xo", 6, 1, 0, "s"),
-    ("px", 7, 0, 0), ("px", 7, 0, 1), ("qd", 2, 1), ("id", 0, 2, "v"), ("xo", 6, 1, 1, "s"), ("xo", 7, 0, 0, "s"),
-    ("sx", 5, 1), ("px", 7, 1, 0), ("sx", 6, 0), ("id", 3, 1, "s"), ("xo", 7, 0, 1, "s"), ("id", 1, 2, "v"),
-    ("xo", 7, 1, 0, "s"), ("px", 7, 1, 1), ("pw", 1, 0, 0, 0), ("sx", 7, 0), ("pw", 0, 0, 0, 0), ("pw", 0, 0, 0, 1),
-    ("xo", 7, 1, 1, "v"), ("qd", 3, 1), ("pw", 0, 1, 0, 0), ("pw", 0, 1, 0, 1), ("sx", 6, 1), ("qd", 0, 2),
-    ("pw", 0, 0, 0, 2), ("id", 2, 2, "v"), ("qd", 1, 2), ("qd", 2, 2), ("id", 3, 2, "s"), ("pw", 2, 1, 0, 0),
-    ("pw", 0, 1, 0, 2), ("pw", 0, 1, 0, 3), ("sx", 7, 1), ("pw", 0, 0, 0, 3), ("wo", 0, 1, 0, "s"),
-    ("pw", 1, 1, 0, 0), ("pw", 1, 0, 0, 1), ("id", 0, 3, "v"), ("id", 2, 3, "v"), ("pw", 1, 0, 0, 2),
-    ("pw", 1, 1, 0, 1), ("pw", 1, 1, 0, 2), ("pw", 1, 0, 0, 3), ("qd", 3, 2), ("wo", 1, 0, 0, "s"),
-    ("pw", 1, 1, 0, 3), ("pw", 2, 0, 0, 0), ("id", 1, 3, "v"), ("wo", 1, 1, 0, "s"), ("pw", 2, 0, 0, 1), ("qd", 1, 3),
-    ("pw", 2, 1, 0, 1), ("pw", 2, 1, 0, 2), ("sw", 1, 0, 0), ("pw", 2, 0, 0, 2), ("id", 3, 3, "s"),
-    ("pw", 2, 0, 0, 3), ("pw", 2, 1, 0, 3), ("qd", 0, 3), ("wo", 2, 0, 0, "s"), ("wo", 0, 0, 0, "s"), ("sw", 1, 1, 0),
-    ("pw", 3, 0, 0, 0), ("ix", 0, 1, "v"), ("pw", 3, 1, 0, 0), ("sw", 0, 1, 0), ("qd", 2, 3), ("sw", 0, 0, 0),
-    ("pw", 3, 1, 0, 1), ("pw", 3, 0, 0, 1), ("pw", 3, 0, 0, 2), ("pw", 3, 1, 0, 2), ("qd", 3, 3), ("sw", 2, 0, 0),
-    ("pw", 3, 0, 0, 3), ("pw", 3, 1, 0, 3), ("wo", 3, 0, 0, "s"), ("qx", 0, 1), ("ix", 1, 1, "v"),
-    ("wo", 3, 1, 0, "v"), ("pw", 3, 1, 1, 0), ("pw", 1, 1, 1, 0), ("sw", 3, 1, 0), ("pw", 0, 0, 1, 0),
-    ("wo", 2, 1, 0, "s"), ("pw", 1, 0, 1, 0), ("pw", 0, 1, 1, 0), ("pw", 2, 0, 1, 0), ("qx", 1, 1),
-    ("pw", 3, 1, 1, 1), ("sw", 2, 1, 0), ("pw", 3, 0, 1, 0), ("ix", 2, 1, "v"), ("pw", 0, 1, 1, 1), ("sw", 3, 0, 0),
-    ("pw", 0, 0, 1, 1), ("ix", 3, 1, "s"), ("qx", 2, 1), ("pw", 1, 0, 1, 1), ("pw", 3, 0, 1, 1), ("pw", 1, 1, 1, 1),
-    ("pw", 2, 1, 1, 0), ("pw", 2, 0, 1, 1), ("qx", 3, 1), ("pw", 0, 1, 1, 2), ("pw", 2, 1, 1, 1), ("pw", 2, 0, 1, 2),
-    ("pw", 2, 1, 1, 2), ("pw", 0, 0, 1, 2), ("pw", 1, 0, 1, 2), ("pw", 0, 0, 1, 3), ("pw", 3, 0, 1, 2),
-    ("pw", 0, 1, 1, 3), ("pw", 1, 1, 1, 2), ("wo", 0, 0, 1, "v"), ("pw", 3, 1, 1, 2), ("wo", 0, 1, 1, "s"),
-    ("sw", 0, 0, 1), ("sw", 0, 1, 1), ("pw", 1, 0, 1, 3), ("pw", 1, 1, 1, 3), ("wo", 1, 1, 1, "v"),
-    ("pw", 2, 0, 1, 3), ("pw", 2, 1, 1, 3), ("wo", 1, 0, 1, "s"), ("wo", 2, 0, 1, "v"), ("pw", 3, 0, 1, 3),
-    ("sw", 1, 0, 1), ("wo", 2, 1, 1, "v"), ("pw", 3, 1, 1, 3), ("sw", 1, 1, 1), ("sw", 2, 1, 1), ("wo", 3, 0, 1, "v"),
-    ("wo", 3, 1, 1, "s"), ("sw", 2, 0, 1), ("sw", 3, 0, 1), ("sw", 3, 1, 1),
-)
+BANK = 512
+CHUNKS = B // (4 * P)
+STEPS = 2 * CHUNKS
+STEP_W = 2 * OUT_F // 4
+PASSES = OUT_F // (4 * P)
+NEGATED = (True, False, False, True)
+Y_AHEAD = 3
+DX_LAG = 2
 
 
 def tile_vdl_v_kernel(tc, x_in, w_in, b_in, y_in, g_in, out_0, out_1):
@@ -96,268 +34,281 @@ def tile_vdl_v_kernel(tc, x_in, w_in, b_in, y_in, g_in, out_0, out_1):
     y_v = y_in.rearrange("(G p j) w -> G p j w", p=P, j=4)
     g_v = g_in.rearrange("(G p j) w -> G p j w", p=P, j=4)
     x_v = x_in.rearrange("(G p j) w -> G p j w", p=P, j=4)
-    w_v = w_in.rearrange("(g q c t a) i -> g c a q t i", g=2, q=16, c=2, t=4, a=4)
-    o0_v = out_0.rearrange("(G p j) i -> G j p i", p=P, j=4)
-    o1_v = out_1.rearrange("(h m a) i -> h a m i", h=2, m=P, a=4)
+    w_v = w_in.rearrange("(g q c t a) i -> g c a q t i", g=PASSES, q=16, c=2, t=4, a=4)
+    dx_v = out_0.rearrange("(G p j) i -> G j p i", p=P, j=4)
+    dw_v = out_1.rearrange("(h m a) i -> h a m i", h=2, m=P, a=4)
 
     with ExitStack() as ctx:
         ctx.enter_context(tc.manual_schedule())
         const = ctx.enter_context(tc.tile_pool(name="const", bufs=1))
-        keep = ctx.enter_context(tc.tile_pool(name="keep", bufs=1))
-        ypool = ctx.enter_context(tc.tile_pool(name="ypool", bufs=3))
-        gpool = ctx.enter_context(tc.tile_pool(name="gpool", bufs=3))
-        xpool = ctx.enter_context(tc.tile_pool(name="xpool", bufs=4))
-        epool = ctx.enter_context(tc.tile_pool(name="epool", bufs=2))
-        dpool = ctx.enter_context(tc.tile_pool(name="dpool", bufs=4))
-        ipool = ctx.enter_context(tc.tile_pool(name="ipool", bufs=3))
-        tpool = ctx.enter_context(tc.tile_pool(name="tpool", bufs=4))
-        cpool = ctx.enter_context(tc.tile_pool(name="cpool", bufs=4))
-        opool = ctx.enter_context(tc.tile_pool(name="opool", bufs=4))
-        qpool = ctx.enter_context(tc.tile_pool(name="qpool", bufs=6))
-        ps = ctx.enter_context(tc.psum_pool(name="ps_all", bufs=8))
+        codes = ctx.enter_context(tc.tile_pool(name="codes", bufs=1))
+        y_pool = ctx.enter_context(tc.tile_pool(name="y_pool", bufs=Y_AHEAD))
+        g_pool = ctx.enter_context(tc.tile_pool(name="g_pool", bufs=Y_AHEAD))
+        xw_pool = ctx.enter_context(tc.tile_pool(name="xw_pool", bufs=3))
+        act_pool = ctx.enter_context(tc.tile_pool(name="act_pool", bufs=2))
+        dy_pool = ctx.enter_context(tc.tile_pool(name="dy_pool", bufs=CHUNKS))
+        il_pool = ctx.enter_context(tc.tile_pool(name="il_pool", bufs=3))
+        tr_pool = ctx.enter_context(tc.tile_pool(name="tr_pool", bufs=4))
+        tc_pool = ctx.enter_context(tc.tile_pool(name="tc_pool", bufs=DX_LAG + 2))
+        dx_pool = ctx.enter_context(tc.tile_pool(name="dx_pool", bufs=4))
+        dw_pool = ctx.enter_context(tc.tile_pool(name="dw_pool", bufs=4))
+        ps_turn = ctx.enter_context(tc.psum_pool(name="ps_turn", bufs=4))
+        ps_hold = ctx.enter_context(tc.psum_pool(name="ps_hold", bufs=4))
 
-        warm = const.tile([P, 1], F32, name="warm")
-        warm2 = const.tile([P, 1], F32, name="warm2")
-        nc.vector.memset(warm[:], 0.0)
-        nc.scalar.activation(out=warm2[:], in_=warm[:], func=ACT.Silu)
+        zero_col = const.tile([P, 1], F32, name="zero_col")
+        unread = const.tile([P, 1], F32, name="unread")
+        nc.vector.memset(zero_col[:], 0.0)
+        nc.scalar.activation(out=unread[:], in_=zero_col[:], func=ACT.Silu)
         ident = const.tile([P, P], F32, name="ident")
         make_identity(nc, ident[:])
-        identb = const.tile([P, P], BF16, name="identb")
-        make_identity(nc, identb[:])
-        pidx = const.tile([P, 1], I32, name="pidx")
-        nc.gpsimd.iota(pidx[:], pattern=[[0, 1]], base=2, channel_multiplier=1)
-        pbit = const.tile([P, 1], I32, name="pbit")
-        nc.vector.tensor_scalar(out=pbit[:], in0=pidx[:], scalar1=1, scalar2=2,
+        p_plus_2 = const.tile([P, 1], I32, name="p_plus_2")
+        nc.gpsimd.iota(p_plus_2[:], pattern=[[0, 1]], base=2, channel_multiplier=1)
+        zero_or_two = const.tile([P, 1], I32, name="zero_or_two")
+        nc.vector.tensor_scalar(out=zero_or_two[:], in0=p_plus_2[:], scalar1=1, scalar2=2,
                                 op0=ALU.logical_shift_right, op1=ALU.bitwise_and)
-        sgn = const.tile([P, 1], F32, name="sgn")
-        nc.vector.tensor_scalar(out=sgn[:], in0=pbit[:], scalar1=-1.0, scalar2=None, op0=ALU.add)
+        w_sign = const.tile([P, 1], F32, name="w_sign")
+        nc.vector.tensor_scalar(out=w_sign[:], in0=zero_or_two[:], scalar1=-1.0, scalar2=None, op0=ALU.add)
 
-        dyc = keep.tile([P, NG, OUT_F], U32, name="dyc", align_bytes=64)
-        dys = keep.tile([P, NG, OUT_F], U8, name="dys", align_bytes=64)
-        xc = keep.tile([P, NG, IN_F], U32, name="xc", align_bytes=64)
-        xs = keep.tile([P, NG, IN_F], U8, name="xs", align_bytes=64)
-        wc = keep.tile([P, 2, IN_F], U32, name="wc", align_bytes=64)
-        ws = keep.tile([P, 2, IN_F], U8, name="ws", align_bytes=64)
+        dy_codes = codes.tile([P, CHUNKS, OUT_F], U32, name="dy_codes", align_bytes=64)
+        dy_scales = codes.tile([P, CHUNKS, OUT_F], U8, name="dy_scales", align_bytes=64)
+        x_codes = codes.tile([P, CHUNKS, IN_F], U32, name="x_codes", align_bytes=64)
+        x_scales = codes.tile([P, CHUNKS, IN_F], U8, name="x_scales", align_bytes=64)
+        w_codes = codes.tile([P, PASSES, IN_F], U32, name="w_codes", align_bytes=64)
+        w_scales = codes.tile([P, PASSES, IN_F], U8, name="w_scales", align_bytes=64)
 
-        held = {}
+        live = {}
 
-        def load_y(s):
+        def half(ih):
+            return slice(BANK * ih, BANK * (ih + 1))
+
+        def load_step(s):
             G, h = divmod(s, 2)
-            yt = ypool.tile([P, 2, OUT_F], F32, name="yt", tag="yt")
-            nc.sync.dma_start(out=yt[:], in_=y_v[G][:, 2 * h:2 * h + 2, :])
-            held[("y", s)] = yt[:].rearrange("p j w -> p (j w)")
-
-        def load_g(s):
-            G, h = divmod(s, 2)
-            gt = gpool.tile([P, 2, OUT_F], BF16, name="gt", tag="gt")
-            nc.sync.dma_start(out=gt[:], in_=g_v[G][:, 2 * h:2 * h + 2, :])
-            held[("g", s)] = gt[:].rearrange("p j w -> p (j w)")
+            y_t = y_pool.tile([P, 2, OUT_F], F32, name="y_t")
+            nc.sync.dma_start(out=y_t[:], in_=y_v[G][:, 2 * h:2 * h + 2, :])
+            g_t = g_pool.tile([P, 2, OUT_F], BF16, name="g_t")
+            nc.sync.dma_start(out=g_t[:], in_=g_v[G][:, 2 * h:2 * h + 2, :])
+            live[("y", s)] = y_t[:].rearrange("p j w -> p (j w)")
+            live[("g", s)] = g_t[:].rearrange("p j w -> p (j w)")
 
         def load_x(G):
-            xt = xpool.tile([P, 4, IN_F], BF16, name="xt", tag="xw")
-            nc.sync.dma_start(out=xt[:], in_=x_v[G])
-            held[("x", G)] = xt
+            x_t = xw_pool.tile([P, 4, IN_F], BF16, name="x_t", tag="xw")
+            nc.sync.dma_start(out=x_t[:], in_=x_v[G])
+            live[("x", G)] = x_t
 
-        def load_w(g, half, queue):
-            if ("w", g) not in held:
-                wt = xpool.tile([P, 4, IN_F], BF16, name="wt", tag="xw")
-                held[("w", g)] = wt
-            for a in (2 * half, 2 * half + 1):
+        def load_w(g):
+            w_t = xw_pool.tile([P, 4, IN_F], BF16, name="w_t", tag="xw")
+            for a in range(4):
+                queue = nc.sync if a < 2 else nc.scalar
                 for c2 in range(2):
-                    (nc.sync if queue == "p" else nc.scalar).dma_start(out=held[("w", g)][2 * a + c2:P:8, :, :],
-                                                                       in_=w_v[g, c2, a])
+                    queue.dma_start(out=w_t[2 * a + c2:P:8, :, :], in_=w_v[g, c2, a])
+            live[("w", g)] = w_t
 
-        def col(flat, a):
-            return flat[:, a:2048:4]
+        def column(flat, a):
+            return flat[:, a:4 * STEP_W:4]
 
         def runs(ap):
             return ap.rearrange("p (n c) -> p n c", c=8)
 
-        def dyn(G):
-            if ("dyn", G) not in held:
-                t = dpool.tile([P, 4, OUT_F], BF16, name="dyn", tag="dyn", align_bytes=64)
-                held[("dyn", G)] = t
-            return held[("dyn", G)]
-
-        def dst(s, a):
+        def dy_runs(s, a):
             G, h = divmod(s, 2)
-            return dyn(G)[:].rearrange("p j w -> p (j w)")[:, 2048 * h:2048 * (h + 1)].rearrange(
-                "p (n a c) -> p a n c", a=4, c=8)[:, a]
+            if ("dy", G) not in live:
+                dy_t = dy_pool.tile([P, 4, OUT_F], BF16, name="dy_t", align_bytes=64)
+                live[("dy", G)] = dy_t
+            flat = live[("dy", G)][:].rearrange("p j w -> p (j w)")
+            return flat[:, 2 * OUT_F * h:2 * OUT_F * (h + 1)].rearrange("p (n a c) -> p a n c", a=4, c=8)[:, a]
 
-        def work(kind, s, dtype):
-            if (kind, s) not in held:
-                t = epool.tile([P, 512], dtype, name=kind, tag=kind)
-                held[(kind, s)] = t
-            return held[(kind, s)]
-
-        def pe_g(s, k):
-            gp = ps.tile([P, 2, 512], BF16, name="gp", tag="bank")
-            held[("gp", s, k)] = gp
-            for a in range(4):
-                if GSLOT[a][0] == k:
-                    nc.tensor.matmul(out=gp[:, GSLOT[a][1], :], lhsT=identb[:], rhs=col(held[("g", s)], a),
-                                     start=True, stop=True)
-
-        def gcol(s, a):
-            k, i = GSLOT[a]
-            return runs(held[("gp", s, k)][:, i, :])
-
-        def v_turns(s):
-            nc.vector.tensor_scalar(out=work("rr", s, F32)[:], in0=col(held[("y", s)], 1), scalar1=1.0 / (2.0 * math.pi),
+        def whole_turns(s):
+            turns = act_pool.tile([P, STEP_W], I32, name="turns")
+            live[("turns", s)] = turns
+            nc.vector.tensor_scalar(out=turns[:], in0=column(live[("y", s)], 1), scalar1=1.0 / (2.0 * math.pi),
                                     scalar2=0.25, op0=ALU.mult, op1=ALU.add)
 
-        def v_whole(s):
-            nc.vector.tensor_copy(out=work("kk", s, I32)[:], in_=work("rr", s, F32)[:])
+        def reduce_angle(s):
+            angle = act_pool.tile([P, STEP_W], F32, name="angle")
+            live[("angle", s)] = angle
+            nc.vector.scalar_tensor_tensor(out=angle[:], in0=live[("turns", s)][:], scalar=-2.0 * math.pi,
+                                           in1=column(live[("y", s)], 1), op0=ALU.mult, op1=ALU.add)
 
-        def v_reduce(s):
-            nc.vector.scalar_tensor_tensor(out=work("rr", s, F32)[:], in0=work("kk", s, I32)[:], scalar=-1.0,
-                                           in1=work("rr", s, F32)[:], op0=ALU.mult, op1=ALU.add)
+        def cosine(s):
+            angle = live[("angle", s)]
+            nc.scalar.activation(out=angle[:], in_=angle[:], func=ACT.Sin, bias=0.5 * math.pi)
 
-        def v_relu(s):
-            nc.vector.scalar_tensor_tensor(out=dst(s, 2), in0=runs(col(held[("y", s)], 2)), scalar=0.0, in1=gcol(s, 2),
-                                           op0=ALU.is_gt, op1=ALU.mult)
+        def tanh(s, a):
+            th = act_pool.tile([P, STEP_W], F32, name="th%d" % a)
+            live[("th", s, a)] = th
+            nc.scalar.activation(out=th[:], in_=column(live[("y", s)], a), func=ACT.Tanh, scale=1.0 if a == 0 else 0.5)
 
-        def s_tanh(s, a):
-            nc.scalar.activation(out=work("t%d" % a, s, F32)[:], in_=col(held[("y", s)], a), func=ACT.Tanh,
-                                 scale=1.0 if a == 0 else 0.5)
+        def square(s, a):
+            th = live[("th", s, a)]
+            nc.scalar.activation(out=th[:], in_=th[:], func=ACT.Square, scale=1.0 if a == 0 else 0.5)
 
-        def s_square(s, a):
-            t = work("t%d" % a, s, F32)
-            nc.scalar.activation(out=t[:], in_=t[:], func=ACT.Square, scale=1.0 if a == 0 else 0.5)
-
-        def s_sin(s):
-            t = work("rr", s, F32)
-            nc.scalar.activation(out=t[:], in_=t[:], func=ACT.Sin, scale=2.0 * math.pi)
-
-        def v_mul(s, a):
+        def times_g(s, a):
+            g_a = runs(column(live[("g", s)], a))
             if a == 1:
-                nc.vector.tensor_tensor(out=dst(s, 1), in0=runs(work("rr", s, F32)[:]), in1=gcol(s, 1), op=ALU.mult)
+                nc.vector.tensor_tensor(out=dy_runs(s, 1), in0=runs(live[("angle", s)][:]), in1=g_a, op=ALU.mult)
+            elif a == 2:
+                nc.vector.scalar_tensor_tensor(out=dy_runs(s, 2), in0=runs(column(live[("y", s)], 2)), scalar=0.0,
+                                               in1=g_a, op0=ALU.is_gt, op1=ALU.mult)
             else:
-                nc.vector.scalar_tensor_tensor(out=dst(s, a), in0=runs(work("t%d" % a, s, F32)[:]),
-                                               scalar=1.0 if a == 0 else 0.25, in1=gcol(s, a),
+                nc.vector.scalar_tensor_tensor(out=dy_runs(s, a), in0=runs(live[("th", s, a)][:]),
+                                               scalar=1.0 if a == 0 else 0.25, in1=g_a,
                                                op0=ALU.subtract, op1=ALU.mult)
 
-        def copy_on(eng, o, i):
-            if eng == "v":
-                nc.vector.tensor_copy(out=o, in_=i)
+        def interleave(what, n, k):
+            width = BANK if what != "dy" else OUT_F // 4
+            il = il_pool.tile([P, 4 * width], BF16, name="il", tag="il_dy" if what == "dy" else "il_xw", align_bytes=64)
+            live[("il", what, n, k)] = il
+            if what == "dy":
+                nc.vector.tensor_copy(
+                    out=il[:].rearrange("p (b c i j) -> p b c j i", b=32, c=2, i=4),
+                    in_=live[("dy", n)][:].rearrange("p j (b a c i) -> p a b c j i", a=4, c=2, i=4)[:, k])
+                return
+            out = il[:].rearrange("p (c i j) -> p c j i", i=4, j=4)
+            rows = live[(what, n)][:, :, half(k)].rearrange("p j (c i) -> p c j i", i=4)
+            if what == "w":
+                nc.vector.tensor_scalar(out=out, in0=rows, scalar1=w_sign[:, 0:1], scalar2=None, op0=ALU.mult)
             else:
-                nc.scalar.copy(out=o, in_=i)
+                nc.vector.tensor_copy(out=out, in_=rows)
 
-        def il_w(g, ih, eng):
-            il = ipool.tile([P, 2048], BF16, name="il", tag="il", align_bytes=64)
-            held[("ilw", g, ih)] = il
-            o = il[:].rearrange("p (c i t) -> p c t i", i=4, t=4)
-            i = held[("w", g)][:, :, 512 * ih:512 * (ih + 1)].rearrange("p t (c i) -> p c t i", i=4)
-            if eng == "v":
-                nc.vector.tensor_scalar(out=o, in0=i, scalar1=sgn[:, 0:1], scalar2=None, op0=ALU.mult)
+        def quantise(what, n, k):
+            il = live[("il", what, n, k)]
+            if what == "dy":
+                cols = slice(256 * k, 256 * (k + 1))
+                nc.vector.quantize_mx(out=dy_codes[:, n, cols].bitcast(E5M2), scales=dy_scales[:, n, cols], in_=il[:])
+            elif what == "w":
+                nc.vector.quantize_mx(out=w_codes[:, n, half(k)].bitcast(E4M3), scales=w_scales[:, n, half(k)], in_=il[:])
             else:
-                nc.scalar.activation(out=o, in_=i, func=ACT.Copy, scale=sgn[:, 0:1])
+                nc.vector.quantize_mx(out=x_codes[:, n, half(k)].bitcast(E4M3), scales=x_scales[:, n, half(k)], in_=il[:])
 
-        def q_w(g, ih):
-            nc.vector.quantize_mx(out=wc[:, g, 512 * ih:512 * (ih + 1)].bitcast(E4),
-                                  scales=ws[:, g, 512 * ih:512 * (ih + 1)], in_=held[("ilw", g, ih)][:])
-
-        def il_x(G, ih, eng):
-            il = ipool.tile([P, 2048], BF16, name="il", tag="il", align_bytes=64)
-            held[("ilx", G, ih)] = il
-            copy_on(eng, il[:].rearrange("p (c i j) -> p c j i", i=4, j=4),
-                    held[("x", G)][:, :, 512 * ih:512 * (ih + 1)].rearrange("p j (c i) -> p c j i", i=4))
-
-        def q_x(G, ih):
-            nc.vector.quantize_mx(out=xc[:, G, 512 * ih:512 * (ih + 1)].bitcast(E4),
-                                  scales=xs[:, G, 512 * ih:512 * (ih + 1)], in_=held[("ilx", G, ih)][:])
-
-        def il_d(G, a, eng):
-            il = ipool.tile([P, 1024], BF16, name="ild", tag="ild", align_bytes=64)
-            held[("ild", G, a)] = il
-            o = il[:].rearrange("p (n c i j) -> p n c j i", n=32, c=2, i=4)
-            i = dyn(G)[:].rearrange("p j (n a c i) -> p a n c j i", a=4, c=2, i=4)[:, a]
-            if eng == "v":
-                nc.vector.tensor_copy(out=o, in_=i)
-            else:
-                for c in range(2):
-                    nc.scalar.copy(out=o[:, :, c], in_=i[:, :, c])
-
-        def q_d(G, a):
-            nc.vector.quantize_mx(out=dyc[:, G, 256 * a:256 * (a + 1)].bitcast(E5),
-                                  scales=dys[:, G, 256 * a:256 * (a + 1)], in_=held[("ild", G, a)][:])
-
-        def pe_flip(s, g):
+        def transpose_step(s, g):
             G, h = divmod(s, 2)
-            tp = ps.tile([P, 2, 2, P], F32, name="tp", tag="bank")
-            held[("tp", s, g)] = tp
+            bank = ps_turn.tile([P, 2, 2, P], F32, name="t_bank", tag="bank")
             for jj in range(2):
-                words = dyn(G)[:, 2 * h + jj, :].bitcast(F32)
+                words = live[("dy", G)][:, 2 * h + jj, :].bitcast(F32)
                 for u in range(2):
-                    nc.tensor.transpose(tp[:, jj, u, :], words[:, 256 * g + u:256 * (g + 1):2], ident[:])
+                    nc.tensor.transpose(bank[:, jj, u, :], words[:, 256 * g + u:256 * (g + 1):2], ident[:])
+            dy_T = tr_pool.tile([P, 4 * 2 * P], BF16, name="dy_T", align_bytes=64)
+            live[("dy_T", s, g)] = dy_T
+            nc.scalar.copy(out=dy_T[:].bitcast(F32).rearrange("p (j r u) -> p j r u", j=2, u=2),
+                           in_=bank[:].rearrange("p j u r -> p j r u"))
 
-        def flip_out(s, g, eng):
-            ti = tpool.tile([P, 1024], BF16, name="ti", tag="ti", align_bytes=64)
-            held[("ti", s, g)] = ti
-            copy_on(eng, ti[:].bitcast(F32).rearrange("p (j r u) -> p j r u", j=2, u=2),
-                    held[("tp", s, g)][:].rearrange("p j u r -> p j r u"))
+        def quantise_transposed(s, g):
+            if g == 0:
+                t_codes = tc_pool.tile([P, PASSES, 2 * P], U32, name="t_codes", align_bytes=64)
+                t_scales = tc_pool.tile([P, PASSES, 2 * P], U8, name="t_scales", align_bytes=64)
+                live[("t_codes", s)] = t_codes
+                live[("t_scales", s)] = t_scales
+            nc.vector.quantize_mx(out=live[("t_codes", s)][:, g, :].bitcast(E5M2), scales=live[("t_scales", s)][:, g, :],
+                                  in_=live[("dy_T", s, g)][:])
 
-        def q_t(s, g):
-            if ("tcd", s) not in held:
-                tcd = cpool.tile([P, 2, 256], U32, name="tcd", tag="tcd", align_bytes=64)
-                tsc = cpool.tile([P, 2, 256], U8, name="tsc", tag="tsc", align_bytes=64)
-                held[("tcd", s)] = tcd
-                held[("tsc", s)] = tsc
-            nc.vector.quantize_mx(out=held[("tcd", s)][:, g, :].bitcast(E5), scales=held[("tsc", s)][:, g, :],
-                                  in_=held[("ti", s, g)][:])
-
-        def pe_dx(s, jj, ih):
-            px = ps.tile([P, 512], F32, name="px", tag="bank")
-            held[("px", s, jj, ih)] = px
-            for g in range(2):
-                nc.tensor.matmul_mx(
-                    out=px[:],
-                    lhsT=held[("tcd", s)][:, g, P * jj:P * (jj + 1)].bitcast(E5),
-                    lhsT_scale=held[("tsc", s)][:, g, P * jj:P * (jj + 1)],
-                    rhs=wc[:, g, 512 * ih:512 * (ih + 1)].bitcast(E4),
-                    rhs_scale=ws[:, g, 512 * ih:512 * (ih + 1)],
-                    start=(g == 0), stop=(g == 1))
-
-        def dx_out(s, jj, ih, eng):
-            if ("ot", s, jj) not in held:
-                ot = opool.tile([P, IN_F], F32, name="ot", tag="ot")
-                held[("ot", s, jj)] = ot
-            copy_on(eng, held[("ot", s, jj)][:, 512 * ih:512 * (ih + 1)], held[("px", s, jj, ih)][:])
-
-        def st_dx(s, jj):
+        def dx_step(s):
             G, h = divmod(s, 2)
-            nc.sync.dma_start(out=o0_v[G, 2 * h + jj], in_=held[("ot", s, jj)][:])
+            for jj in range(2):
+                rows = dx_pool.tile([P, IN_F], F32, name="dx_rows")
+                tokens = slice(P * jj, P * (jj + 1))
+                for ih in range(2):
+                    acc = ps_turn.tile([P, BANK], F32, name="dx_acc", tag="bank")
+                    for g in range(PASSES):
+                        nc.tensor.matmul_mx(
+                            out=acc[:],
+                            lhsT=live[("t_codes", s)][:, g, tokens].bitcast(E5M2),
+                            lhsT_scale=live[("t_scales", s)][:, g, tokens],
+                            rhs=w_codes[:, g, half(ih)].bitcast(E4M3),
+                            rhs_scale=w_scales[:, g, half(ih)],
+                            start=(g == 0), stop=(g == PASSES - 1))
+                    nc.scalar.copy(out=rows[:, half(ih)], in_=acc[:])
+                nc.sync.dma_start(out=dx_v[G, 2 * h + jj], in_=rows[:])
 
-        def dw_pass(a, h, ih, G):
-            if ("pw", a, h, ih) not in held:
-                pw = ps.tile([P, 512], F32, name="pw", tag="bank")
-                held[("pw", a, h, ih)] = pw
-            lo = 256 * a + P * h
-            nc.tensor.matmul_mx(
-                out=held[("pw", a, h, ih)][:],
-                lhsT=dyc[:, G, lo:lo + P].bitcast(E5),
-                lhsT_scale=dys[:, G, lo:lo + P],
-                rhs=xc[:, G, 512 * ih:512 * (ih + 1)].bitcast(E4),
-                rhs_scale=xs[:, G, 512 * ih:512 * (ih + 1)],
-                start=(G == 0), stop=(G == NG - 1))
+        def dw_passes(a, G):
+            for h in range(2):
+                feats = slice(256 * a + P * h, 256 * a + P * (h + 1))
+                for ih in range(2):
+                    if G == 0:
+                        acc = (ps_hold if a % 2 == 0 else ps_turn).tile([P, BANK], F32, name="dw_acc", tag="bank")
+                        live[("dw", a, h, ih)] = acc
+                    nc.tensor.matmul_mx(
+                        out=live[("dw", a, h, ih)][:],
+                        lhsT=dy_codes[:, G, feats].bitcast(E5M2),
+                        lhsT_scale=dy_scales[:, G, feats],
+                        rhs=x_codes[:, G, half(ih)].bitcast(E4M3),
+                        rhs_scale=x_scales[:, G, half(ih)],
+                        start=(G == 0), stop=(G == CHUNKS - 1))
 
-        def dw_out(a, h, ih, eng):
-            qt = qpool.tile([P, 512], F32, name="qt", tag="qt")
-            held[("qt", a, h, ih)] = qt
-            i = held[("pw", a, h, ih)][:]
-            if not NEG[a]:
-                copy_on(eng, qt[:], i)
-            elif eng == "v":
-                nc.vector.tensor_scalar(out=qt[:], in0=i, scalar1=-1.0, scalar2=None, op0=ALU.mult)
-            else:
-                nc.scalar.activation(out=qt[:], in_=i, func=ACT.Copy, scale=-1.0)
+        def dw_store(a, share):
+            for h in range(2):
+                for ih in range(2):
+                    acc = live[("dw", a, h, ih)]
+                    bank = dw_pool.tile([P, BANK], F32, name="dw_bank")
+                    if share and ih == 1:
+                        nc.vector.tensor_scalar(out=bank[:], in0=acc[:], scalar1=-1.0 if NEGATED[a] else 1.0,
+                                                scalar2=None, op0=ALU.mult)
+                    elif NEGATED[a]:
+                        nc.scalar.activation(out=bank[:], in_=acc[:], func=ACT.Copy, scale=-1.0)
+                    else:
+                        nc.scalar.copy(out=bank[:], in_=acc[:])
+                    nc.sync.dma_start(out=dw_v[h, a][:, half(ih)], in_=bank[:])
 
-        def st_dw(a, h, ih):
-            nc.sync.dma_start(out=o1_v[h, a][:, 512 * ih:512 * (ih + 1)], in_=held[("qt", a, h, ih)][:])
+        extra = {1: (("w", 0, 0), ("w", 0, 1)), 2: (("w", 1, 0), ("w", 1, 1)), 3: (("x", 1, 0),), 4: (("x", 1, 1),),
+                 5: (("x", 2, 0),), 6: (("x", 2, 1),), 7: (("x", 3, 0),), 8: (("x", 3, 1),)}
+        x_after = {1: 2, 3: 3}
 
-        fns = {"ly": load_y, "lg": load_g, "lx": load_x, "lw": load_w, "pg": pe_g, "vt": v_turns, "vw": v_whole,
-               "vr": v_reduce, "vl": v_relu, "sh": s_tanh, "sq": s_square, "ss": s_sin, "vm": v_mul,
-               "iw": il_w, "qw": q_w, "ix": il_x, "qx": q_x, "id": il_d, "qd": q_d, "pf": pe_flip, "fo": flip_out,
-               "qt": q_t, "px": pe_dx, "xo": dx_out, "sx": st_dx, "pw": dw_pass, "wo": dw_out, "sw": st_dw}
-        for t in TASKS:
-            fns[t[0]](*t[1:])
+        load_x(0)
+        for s in range(Y_AHEAD):
+            load_step(s)
+        for g in range(PASSES):
+            load_w(g)
+        load_x(1)
+        for ih in range(2):
+            interleave("x", 0, ih)
+        for ih in range(2):
+            quantise("x", 0, ih)
+
+        for s in range(STEPS + DX_LAG):
+            if s < STEPS:
+                whole_turns(s)
+                tanh(s, 0)
+                tanh(s, 3)
+                times_g(s, 2)
+                reduce_angle(s)
+                square(s, 0)
+                square(s, 3)
+                cosine(s)
+            if 1 <= s <= STEPS:
+                for g in range(PASSES):
+                    transpose_step(s - 1, g)
+            for item in extra.get(s, ()):
+                interleave(*item)
+            if s < STEPS:
+                times_g(s, 0)
+                times_g(s, 3)
+            for item in extra.get(s, ()):
+                quantise(*item)
+            if s < STEPS:
+                times_g(s, 1)
+            if s + Y_AHEAD < STEPS:
+                load_step(s + Y_AHEAD)
+            if s in x_after:
+                load_x(x_after[s])
+            if 1 <= s <= STEPS:
+                for g in range(PASSES):
+                    quantise_transposed(s - 1, g)
+            chunk_done = s >= 2 and s % 2 == 0 and s <= STEPS
+            if chunk_done:
+                interleave("dy", s // 2 - 1, 0)
+            if s >= DX_LAG:
+                dx_step(s - DX_LAG)
+            if chunk_done:
+                quantise("dy", s // 2 - 1, 0)
+                dw_passes(0, s // 2 - 1)
+        dw_store(0, False)
+
+        pieces = [(G, a) for a in range(1, 4) for G in range(CHUNKS)]
+        interleave("dy", pieces[0][0], pieces[0][1])
+        for n in range(len(pieces)):
+            G, a = pieces[n]
+            if n + 1 < len(pieces):
+                interleave("dy", pieces[n + 1][0], pieces[n + 1][1])
+            quantise("dy", G, a)
+            dw_passes(a, G)
+            if G == CHUNKS - 1:
+                dw_store(a, a == 3)

@@ -25,7 +25,7 @@ STEPS = 2 * CHUNKS
 STEP_W = 2 * OUT_F // 4
 PASSES = OUT_F // (4 * P)
 NEGATED = (True, False, False, True)
-Y_AHEAD = 3
+Y_AHEAD = 4
 DX_LAG = 2
 
 
@@ -98,9 +98,8 @@ def tile_vdl_v_kernel(tc, x_in, w_in, b_in, y_in, g_in, out_0, out_1):
         def load_w(g):
             w_t = xw_pool.tile([P, 4, IN_F], BF16, name="w_t", tag="xw")
             for a in range(4):
-                queue = nc.sync if a < 2 else nc.scalar
                 for c2 in range(2):
-                    queue.dma_start(out=w_t[2 * a + c2:P:8, :, :], in_=w_v[g, c2, a])
+                    nc.sync.dma_start(out=w_t[2 * a + c2:P:8, :, :], in_=w_v[g, c2, a])
             live[("w", g)] = w_t
 
         def column(flat, a):
@@ -248,15 +247,16 @@ def tile_vdl_v_kernel(tc, x_in, w_in, b_in, y_in, g_in, out_0, out_1):
                         nc.scalar.copy(out=bank[:], in_=acc[:])
                     nc.sync.dma_start(out=dw_v[h, a][:, half(ih)], in_=bank[:])
 
-        extra = {1: (("w", 0, 0), ("w", 0, 1)), 2: (("w", 1, 0), ("w", 1, 1)), 3: (("x", 1, 0),), 4: (("x", 1, 1),),
-                 5: (("x", 2, 0),), 6: (("x", 2, 1),), 7: (("x", 3, 0),), 8: (("x", 3, 1),)}
+        extra = {0: (("w", 0, 0), ("w", 0, 1)), 1: (("w", 1, 0), ("w", 1, 1)), 2: (("x", 1, 0),), 3: (("x", 1, 1),),
+                 4: (("x", 2, 0),), 5: (("x", 2, 1),), 6: (("x", 3, 0),), 7: (("x", 3, 1),)}
         x_after = {1: 2, 3: 3}
 
         load_x(0)
-        for s in range(Y_AHEAD):
-            load_step(s)
+        load_step(0)
         for g in range(PASSES):
             load_w(g)
+        for s in range(1, Y_AHEAD):
+            load_step(s)
         load_x(1)
         for ih in range(2):
             interleave("x", 0, ih)

from contextlib import ExitStack
import math

import concourse.mybir as mybir
from concourse.masks import make_identity

B, IN_F, OUT_F = 2048, 1024, 1024
FLOPS = 2 * 2 * B * IN_F * OUT_F
BYTES = 2 * B * IN_F + 2 * OUT_F * IN_F + 4 * B * OUT_F + 2 * B * OUT_F + 4 * B * IN_F + 4 * OUT_F * IN_F

F32 = mybir.dt.float32
BF16 = mybir.dt.bfloat16
I32 = mybir.dt.int32
U32 = mybir.dt.uint32
U8 = mybir.dt.uint8
E4M3 = mybir.dt.float8_e4m3fn_x4
E5M2 = mybir.dt.float8_e5m2_x4
ACT = mybir.ActivationFunctionType
ALU = mybir.AluOpType

P = 128
BANK = 512
CHUNKS = B // (4 * P)
STEPS = 2 * CHUNKS
STEP_W = 2 * OUT_F // 4
PASSES = OUT_F // (4 * P)
NEGATED = (True, False, False, True)
Y_AHEAD = 4
DX_LAG = 2


def tile_vdl_v_kernel(tc, x_in, w_in, b_in, y_in, g_in, out_0, out_1):
    nc = tc.nc
    y_v = y_in.rearrange("(G p j) w -> G p j w", p=P, j=4)
    g_v = g_in.rearrange("(G p j) w -> G p j w", p=P, j=4)
    x_v = x_in.rearrange("(G p j) w -> G p j w", p=P, j=4)
    w_v = w_in.rearrange("(g q c t a) i -> g c a q t i", g=PASSES, q=16, c=2, t=4, a=4)
    dx_v = out_0.rearrange("(G p j) i -> G j p i", p=P, j=4)
    dw_v = out_1.rearrange("(h m a) i -> h a m i", h=2, m=P, a=4)

    with ExitStack() as ctx:
        ctx.enter_context(tc.manual_schedule())
        const = ctx.enter_context(tc.tile_pool(name="const", bufs=1))
        codes = ctx.enter_context(tc.tile_pool(name="codes", bufs=1))
        y_pool = ctx.enter_context(tc.tile_pool(name="y_pool", bufs=Y_AHEAD))
        g_pool = ctx.enter_context(tc.tile_pool(name="g_pool", bufs=Y_AHEAD))
        xw_pool = ctx.enter_context(tc.tile_pool(name="xw_pool", bufs=3))
        act_pool = ctx.enter_context(tc.tile_pool(name="act_pool", bufs=2))
        dy_pool = ctx.enter_context(tc.tile_pool(name="dy_pool", bufs=CHUNKS))
        il_pool = ctx.enter_context(tc.tile_pool(name="il_pool", bufs=3))
        tr_pool = ctx.enter_context(tc.tile_pool(name="tr_pool", bufs=4))
        tc_pool = ctx.enter_context(tc.tile_pool(name="tc_pool", bufs=DX_LAG + 2))
        dx_pool = ctx.enter_context(tc.tile_pool(name="dx_pool", bufs=4))
        dw_pool = ctx.enter_context(tc.tile_pool(name="dw_pool", bufs=4))
        ps_turn = ctx.enter_context(tc.psum_pool(name="ps_turn", bufs=4))
        ps_hold = ctx.enter_context(tc.psum_pool(name="ps_hold", bufs=4))

        zero_col = const.tile([P, 1], F32, name="zero_col")
        unread = const.tile([P, 1], F32, name="unread")
        nc.vector.memset(zero_col[:], 0.0)
        nc.scalar.activation(out=unread[:], in_=zero_col[:], func=ACT.Silu)
        ident = const.tile([P, P], F32, name="ident")
        make_identity(nc, ident[:])
        p_plus_2 = const.tile([P, 1], I32, name="p_plus_2")
        nc.gpsimd.iota(p_plus_2[:], pattern=[[0, 1]], base=2, channel_multiplier=1)
        zero_or_two = const.tile([P, 1], I32, name="zero_or_two")
        nc.vector.tensor_scalar(out=zero_or_two[:], in0=p_plus_2[:], scalar1=1, scalar2=2,
                                op0=ALU.logical_shift_right, op1=ALU.bitwise_and)
        w_sign = const.tile([P, 1], F32, name="w_sign")
        nc.vector.tensor_scalar(out=w_sign[:], in0=zero_or_two[:], scalar1=-1.0, scalar2=None, op0=ALU.add)

        dy_codes = codes.tile([P, CHUNKS, OUT_F], U32, name="dy_codes", align_bytes=64)
        dy_scales = codes.tile([P, CHUNKS, OUT_F], U8, name="dy_scales", align_bytes=64)
        x_codes = codes.tile([P, CHUNKS, IN_F], U32, name="x_codes", align_bytes=64)
        x_scales = codes.tile([P, CHUNKS, IN_F], U8, name="x_scales", align_bytes=64)
        w_codes = codes.tile([P, PASSES, IN_F], U32, name="w_codes", align_bytes=64)
        w_scales = codes.tile([P, PASSES, IN_F], U8, name="w_scales", align_bytes=64)

        live = {}

        def half(ih):
            return slice(BANK * ih, BANK * (ih + 1))

        def load_step(s):
            G, h = divmod(s, 2)
            y_t = y_pool.tile([P, 2, OUT_F], F32, name="y_t")
            nc.sync.dma_start(out=y_t[:], in_=y_v[G][:, 2 * h:2 * h + 2, :])
            g_t = g_pool.tile([P, 2, OUT_F], BF16, name="g_t")
            nc.sync.dma_start(out=g_t[:], in_=g_v[G][:, 2 * h:2 * h + 2, :])
            live[("y", s)] = y_t[:].rearrange("p j w -> p (j w)")
            live[("g", s)] = g_t[:].rearrange("p j w -> p (j w)")

        def load_x(G):
            x_t = xw_pool.tile([P, 4, IN_F], BF16, name="x_t", tag="xw")
            nc.sync.dma_start(out=x_t[:], in_=x_v[G])
            live[("x", G)] = x_t

        def load_w(g):
            w_t = xw_pool.tile([P, 4, IN_F], BF16, name="w_t", tag="xw")
            for a in range(4):
                for c2 in range(2):
                    nc.sync.dma_start(out=w_t[2 * a + c2:P:8, :, :], in_=w_v[g, c2, a])
            live[("w", g)] = w_t

        def column(flat, a):
            return flat[:, a:4 * STEP_W:4]

        def runs(ap):
            return ap.rearrange("p (n c) -> p n c", c=8)

        def dy_runs(s, a):
            G, h = divmod(s, 2)
            if ("dy", G) not in live:
                dy_t = dy_pool.tile([P, 4, OUT_F], BF16, name="dy_t", align_bytes=64)
                live[("dy", G)] = dy_t
            flat = live[("dy", G)][:].rearrange("p j w -> p (j w)")
            return flat[:, 2 * OUT_F * h:2 * OUT_F * (h + 1)].rearrange("p (n a c) -> p a n c", a=4, c=8)[:, a]

        def whole_turns(s):
            turns = act_pool.tile([P, STEP_W], I32, name="turns")
            live[("turns", s)] = turns
            nc.vector.tensor_scalar(out=turns[:], in0=column(live[("y", s)], 1), scalar1=1.0 / (2.0 * math.pi),
                                    scalar2=0.25, op0=ALU.mult, op1=ALU.add)

        def reduce_angle(s):
            angle = act_pool.tile([P, STEP_W], F32, name="angle")
            live[("angle", s)] = angle
            nc.vector.scalar_tensor_tensor(out=angle[:], in0=live[("turns", s)][:], scalar=-2.0 * math.pi,
                                           in1=column(live[("y", s)], 1), op0=ALU.mult, op1=ALU.add)

        def cosine(s):
            angle = live[("angle", s)]
            nc.scalar.activation(out=angle[:], in_=angle[:], func=ACT.Sin, bias=0.5 * math.pi)

        def tanh(s, a):
            th = act_pool.tile([P, STEP_W], F32, name="th%d" % a)
            live[("th", s, a)] = th
            nc.scalar.activation(out=th[:], in_=column(live[("y", s)], a), func=ACT.Tanh, scale=1.0 if a == 0 else 0.5)

        def square(s, a):
            th = live[("th", s, a)]
            nc.scalar.activation(out=th[:], in_=th[:], func=ACT.Square, scale=1.0 if a == 0 else 0.5)

        def times_g(s, a):
            g_a = runs(column(live[("g", s)], a))
            if a == 1:
                nc.vector.tensor_tensor(out=dy_runs(s, 1), in0=runs(live[("angle", s)][:]), in1=g_a, op=ALU.mult)
            elif a == 2:
                nc.vector.scalar_tensor_tensor(out=dy_runs(s, 2), in0=runs(column(live[("y", s)], 2)), scalar=0.0,
                                               in1=g_a, op0=ALU.is_gt, op1=ALU.mult)
            else:
                nc.vector.scalar_tensor_tensor(out=dy_runs(s, a), in0=runs(live[("th", s, a)][:]),
                                               scalar=1.0 if a == 0 else 0.25, in1=g_a,
                                               op0=ALU.subtract, op1=ALU.mult)

        def interleave(what, n, k):
            width = BANK if what != "dy" else OUT_F // 4
            il = il_pool.tile([P, 4 * width], BF16, name="il", tag="il_dy" if what == "dy" else "il_xw", align_bytes=64)
            live[("il", what, n, k)] = il
            if what == "dy":
                nc.vector.tensor_copy(
                    out=il[:].rearrange("p (b c i j) -> p b c j i", b=32, c=2, i=4),
                    in_=live[("dy", n)][:].rearrange("p j (b a c i) -> p a b c j i", a=4, c=2, i=4)[:, k])
                return
            out = il[:].rearrange("p (c i j) -> p c j i", i=4, j=4)
            rows = live[(what, n)][:, :, half(k)].rearrange("p j (c i) -> p c j i", i=4)
            if what == "w":
                nc.vector.tensor_scalar(out=out, in0=rows, scalar1=w_sign[:, 0:1], scalar2=None, op0=ALU.mult)
            else:
                nc.vector.tensor_copy(out=out, in_=rows)

        def quantise(what, n, k):
            il = live[("il", what, n, k)]
            if what == "dy":
                cols = slice(256 * k, 256 * (k + 1))
                nc.vector.quantize_mx(out=dy_codes[:, n, cols].bitcast(E5M2), scales=dy_scales[:, n, cols], in_=il[:])
            elif what == "w":
                nc.vector.quantize_mx(out=w_codes[:, n, half(k)].bitcast(E4M3), scales=w_scales[:, n, half(k)], in_=il[:])
            else:
                nc.vector.quantize_mx(out=x_codes[:, n, half(k)].bitcast(E4M3), scales=x_scales[:, n, half(k)], in_=il[:])

        def transpose_step(s, g):
            G, h = divmod(s, 2)
            bank = ps_turn.tile([P, 2, 2, P], F32, name="t_bank", tag="bank")
            for jj in range(2):
                words = live[("dy", G)][:, 2 * h + jj, :].bitcast(F32)
                for u in range(2):
                    nc.tensor.transpose(bank[:, jj, u, :], words[:, 256 * g + u:256 * (g + 1):2], ident[:])
            dy_T = tr_pool.tile([P, 4 * 2 * P], BF16, name="dy_T", align_bytes=64)
            live[("dy_T", s, g)] = dy_T
            nc.scalar.copy(out=dy_T[:].bitcast(F32).rearrange("p (j r u) -> p j r u", j=2, u=2),
                           in_=bank[:].rearrange("p j u r -> p j r u"))

        def quantise_transposed(s, g):
            if g == 0:
                t_codes = tc_pool.tile([P, PASSES, 2 * P], U32, name="t_codes", align_bytes=64)
                t_scales = tc_pool.tile([P, PASSES, 2 * P], U8, name="t_scales", align_bytes=64)
                live[("t_codes", s)] = t_codes
                live[("t_scales", s)] = t_scales
            nc.vector.quantize_mx(out=live[("t_codes", s)][:, g, :].bitcast(E5M2), scales=live[("t_scales", s)][:, g, :],
                                  in_=live[("dy_T", s, g)][:])

        def dx_step(s):
            G, h = divmod(s, 2)
            for jj in range(2):
                rows = dx_pool.tile([P, IN_F], F32, name="dx_rows")
                tokens = slice(P * jj, P * (jj + 1))
                for ih in range(2):
                    acc = ps_turn.tile([P, BANK], F32, name="dx_acc", tag="bank")
                    for g in range(PASSES):
                        nc.tensor.matmul_mx(
                            out=acc[:],
                            lhsT=live[("t_codes", s)][:, g, tokens].bitcast(E5M2),
                            lhsT_scale=live[("t_scales", s)][:, g, tokens],
                            rhs=w_codes[:, g, half(ih)].bitcast(E4M3),
                            rhs_scale=w_scales[:, g, half(ih)],
                            start=(g == 0), stop=(g == PASSES - 1))
                    nc.scalar.copy(out=rows[:, half(ih)], in_=acc[:])
                nc.sync.dma_start(out=dx_v[G, 2 * h + jj], in_=rows[:])

        def dw_passes(a, G):
            for h in range(2):
                feats = slice(256 * a + P * h, 256 * a + P * (h + 1))
                for ih in range(2):
                    if G == 0:
                        acc = (ps_hold if a % 2 == 0 else ps_turn).tile([P, BANK], F32, name="dw_acc", tag="bank")
                        live[("dw", a, h, ih)] = acc
                    nc.tensor.matmul_mx(
                        out=live[("dw", a, h, ih)][:],
                        lhsT=dy_codes[:, G, feats].bitcast(E5M2),
                        lhsT_scale=dy_scales[:, G, feats],
                        rhs=x_codes[:, G, half(ih)].bitcast(E4M3),
                        rhs_scale=x_scales[:, G, half(ih)],
                        start=(G == 0), stop=(G == CHUNKS - 1))

        def dw_store(a, share):
            for h in range(2):
                for ih in range(2):
                    acc = live[("dw", a, h, ih)]
                    bank = dw_pool.tile([P, BANK], F32, name="dw_bank")
                    if share and ih == 1:
                        nc.vector.tensor_scalar(out=bank[:], in0=acc[:], scalar1=-1.0 if NEGATED[a] else 1.0,
                                                scalar2=None, op0=ALU.mult)
                    elif NEGATED[a]:
                        nc.scalar.activation(out=bank[:], in_=acc[:], func=ACT.Copy, scale=-1.0)
                    else:
                        nc.scalar.copy(out=bank[:], in_=acc[:])
                    nc.sync.dma_start(out=dw_v[h, a][:, half(ih)], in_=bank[:])

        extra = {0: (("w", 0, 0), ("w", 0, 1)), 1: (("w", 1, 0), ("w", 1, 1)), 2: (("x", 1, 0),), 3: (("x", 1, 1),),
                 4: (("x", 2, 0),), 5: (("x", 2, 1),), 6: (("x", 3, 0),), 7: (("x", 3, 1),)}
        x_after = {1: 2, 3: 3}

        load_x(0)
        load_step(0)
        for g in range(PASSES):
            load_w(g)
        for s in range(1, Y_AHEAD):
            load_step(s)
        load_x(1)
        for ih in range(2):
            interleave("x", 0, ih)
        for ih in range(2):
            quantise("x", 0, ih)

        for s in range(STEPS + DX_LAG):
            if s < STEPS:
                whole_turns(s)
                tanh(s, 0)
                tanh(s, 3)
                times_g(s, 2)
                reduce_angle(s)
                square(s, 0)
                square(s, 3)
                cosine(s)
            if 1 <= s <= STEPS:
                for g in range(PASSES):
                    transpose_step(s - 1, g)
            for item in extra.get(s, ()):
                interleave(*item)
            if s < STEPS:
                times_g(s, 0)
                times_g(s, 3)
            for item in extra.get(s, ()):
                quantise(*item)
            if s < STEPS:
                times_g(s, 1)
            if s + Y_AHEAD < STEPS:
                load_step(s + Y_AHEAD)
            if s in x_after:
                load_x(x_after[s])
            if 1 <= s <= STEPS:
                for g in range(PASSES):
                    quantise_transposed(s - 1, g)
            chunk_done = s >= 2 and s % 2 == 0 and s <= STEPS
            if chunk_done:
                interleave("dy", s // 2 - 1, 0)
            if s >= DX_LAG:
                dx_step(s - DX_LAG)
            if chunk_done:
                quantise("dy", s // 2 - 1, 0)
                dw_passes(0, s // 2 - 1)
        dw_store(0, False)

        pieces = [(G, a) for a in range(1, 4) for G in range(CHUNKS)]
        interleave("dy", pieces[0][0], pieces[0][1])
        for n in range(len(pieces)):
            G, a = pieces[n]
            if n + 1 < len(pieces):
                interleave("dy", pieces[n + 1][0], pieces[n + 1][1])
            quantise("dy", G, a)
            dw_passes(a, G)
            if G == CHUNKS - 1:
                dw_store(a, a == 3)
